import numpy as np
import ml_dtypes


def mxq(x, axis, fmt="e4m3"):
    dtype, down = {"e4m3": (ml_dtypes.float8_e4m3fn, 7), "e5m2": (ml_dtypes.float8_e5m2, 14)}[fmt]
    v = np.moveaxis(np.asarray(x, np.float32).astype(ml_dtypes.bfloat16).astype(np.float64), axis, -1)
    blocks = v.reshape(v.shape[:-1] + (-1, 32))
    amax = np.abs(blocks).max(-1, keepdims=True)
    byte = np.maximum(np.where(amax > 0, np.frexp(amax)[1] - 1 + 127, 0) - down, 1)
    scale = np.exp2(byte - 127.0)
    codes = (blocks / scale).astype(np.float32).astype(dtype).astype(np.float64)
    return np.moveaxis((codes * scale).reshape(v.shape), -1, axis)


WIDE = False


def mx_kscale(k):
    if not WIDE:
        return np.ones(k)
    levels = np.array([10, -10, 5, -5, 0])
    a = np.random.permutation(np.resize(levels, k // 512 * 4)).reshape(k // 512, 4)
    idx = np.arange(k)
    return np.exp2(a[idx // 512, idx % 128 // 32])


BF16 = ml_dtypes.bfloat16


def bf(x):
    return np.asarray(x, np.float32).astype(BF16)


def f64(x):
    return np.asarray(x).astype(np.float64)


E2M1 = np.array([0.0, 0.5, 1.0, 1.5, 2.0, 3.0, 4.0, 6.0, -0.0, -0.5, -1.0, -1.5, -2.0, -3.0, -4.0, -6.0])


def pack_weight(w, fmt):
    k, n = w.shape
    w = f64(bf(w)).reshape(k // 32, 32, n)
    amax = np.abs(w).max(1)
    if fmt == "e4m3":
        byte = np.frexp(amax)[1] - 1 + 127 - 7
    else:
        mant, ex = np.frexp(amax / 6.0)
        byte = np.where(mant > 0.5, ex, ex - 1) + 127
    byte = np.clip(np.where(amax > 0, byte, 1), 1, 254)
    scaled = (w * np.exp2(127.0 - byte)[:, None, :]).reshape(k, n).astype(np.float32)
    by_word = np.ascontiguousarray(scaled.reshape(k // 512, 128, 4, n).transpose(0, 1, 3, 2))
    if fmt == "e4m3":
        words = by_word.astype(ml_dtypes.float8_e4m3fn).view(np.uint8)
    else:
        c = by_word.astype(ml_dtypes.float4_e2m1fn).view(np.uint8) & 0xF
        words = c[..., 0::2] | (c[..., 1::2] << 4)
    return np.ascontiguousarray(words), np.ascontiguousarray(byte.astype(np.uint8).reshape(k // 512, 16, n))


def unpack_weight(words, scales, fmt):
    g, p, n, _ = words.shape
    if fmt == "e4m3":
        vals = np.ascontiguousarray(words).view(ml_dtypes.float8_e4m3fn).astype(np.float64)
    else:
        nib = np.empty((g, p, n, 4), np.uint8)
        nib[..., 0::2] = words & 0xF
        nib[..., 1::2] = words >> 4
        vals = E2M1[nib]
    vals = vals * np.repeat(np.exp2(scales.astype(np.float64) - 127.0), 8, axis=1)[..., None]
    return vals.transpose(0, 1, 3, 2).reshape(g * 512, n)

def pack4(w):
    words, scales = pack_weight(w, "e2m1")
    return words.reshape(words.shape[0], 128, -1), scales


def unpack4(words, scales):
    return unpack_weight(words.reshape(words.shape[0], 128, -1, 2), scales, "e2m1")


B, N, C0, C1, C2, O0, O1, O2 = 16, 16, 512, 512, 512, 512, 2048, 512
P = C0 + C1
K = P + 2 * C2


def sigmoid(v):
    return 1.0 / (1.0 + np.exp(-v))


def setup_inputs():
    s = mx_kscale(K)[:P]
    lo = 0.4 * np.random.random((B, N, 1, C2))
    hi = 1.0 - 0.4 * np.random.random((B, N, 1, C2))
    x2 = lo + (hi - lo) * np.random.random((B, N, N, C2))
    i = np.arange(N)
    x2[:, i, i, :] = np.random.random((B, N, C2)) < 0.5
    w = np.random.standard_normal((K, O1)) * 2.0 / np.sqrt(K)
    w[:P] = w[:P] / s[:, None]
    words, scales = pack4(w)
    return {"x0": bf(np.random.random((B, C0)) * s[:C0]),
            "x1": bf(np.random.random((B, N, C1)) * s[C0:]),
            "x2": bf(x2),
            "W1_words": words,
            "W1_scales": scales,
            "b1": bf(np.random.standard_normal(O1) * 0.3)}


def reference(x0, x1, x2, W1_words, W1_scales, b1):
    x0, x1, x2 = f64(x0), f64(x1), f64(x2)
    e0 = np.broadcast_to(x0[:, None, :], (B, N, C0))
    diag = np.eye(N, dtype=bool)[None, :, :, None]
    rmax = np.where(diag, 0.0, x2).max(axis=2)
    rmin = np.where(diag, 1.0, x2).min(axis=2)
    f1 = np.concatenate([e0, x1, rmax, rmin], axis=-1)
    return sigmoid((mxq(f1, 2, "e4m3") @ unpack4(W1_words, W1_scales)) + f64(b1))

@@ -1,0 +1,221 @@
+from contextlib import ExitStack
+
+import concourse.mybir as mybir
+from concourse.masks import make_identity
+
+BF16 = mybir.dt.bfloat16
+F32 = mybir.dt.float32
+I32 = mybir.dt.int32
+U8 = mybir.dt.uint8
+U32 = mybir.dt.uint32
+FP8X4 = mybir.dt.float8_e4m3fn_x4
+FP4X4 = mybir.dt.float4_e2m1fn_x4
+ALU = mybir.AluOpType
+ACT = mybir.ActivationFunctionType
+
+P = 128
+SCENES = 16
+OBJECTS = 16
+CH = 512
+OUT = 2048
+PACK = 4
+WORD_HALVES = 2
+GROUPS = 4
+TILE_SCENES = P // OBJECTS
+TOKEN_TILES = SCENES // TILE_SCENES
+QUARTER = 4
+QUARTERS = OBJECTS // QUARTER
+BANK_ROWS = 2
+N_TILE = 512
+N_TILES = OUT // N_TILE
+OBJECT_WORDS = TILE_SCENES * WORD_HALVES
+
+FLOPS = 2 * SCENES * OBJECTS * GROUPS * CH * OUT
+
+REDUCTIONS = ((ALU.max, 0.0), (ALU.min, 1.0))
+
+
+def to_channel_major(nc, banks, identity, src, dst):
+    words = banks.tile([P, BANK_ROWS, WORD_HALVES, P], F32, tag="bank")
+    for s in range(BANK_ROWS):
+        src_words = src[:, s, :].bitcast(F32)
+        for u in range(WORD_HALVES):
+            nc.tensor.transpose(words[:, s, u, :], src_words[:, u : CH // 2 : WORD_HALVES], identity)
+    nc.scalar.copy(
+        out=dst.bitcast(F32).rearrange("p s (k u) -> p s k u", u=WORD_HALVES),
+        in_=words[:].rearrange("p s u k -> p s k u"),
+    )
+
+
+def tile_differentiablelogicmachine_pb_kernel(tc, x0, x1, x2, W1_words, W1_scales, b1, out):
+    nc = tc.nc
+    with ExitStack() as stack:
+        keep = stack.enter_context(tc.tile_pool(name="keep", bufs=1))
+        work = stack.enter_context(tc.tile_pool(name="work", bufs=2))
+        results = stack.enter_context(tc.tile_pool(name="results", bufs=4))
+        banks = stack.enter_context(tc.psum_pool(name="banks", bufs=8))
+        stack.enter_context(tc.manual_schedule())
+
+        def scenes(t):
+            return slice(t * TILE_SCENES, (t + 1) * TILE_SCENES)
+
+        bias_row = keep.tile([P, OUT], BF16)
+        nc.vector.memset(bias_row[:].bitcast(I32), 0)
+        nc.scalar.dma_start(out=bias_row[0:1, :], in_=b1.rearrange("(o n) -> o n", o=1))
+        w_scales = keep.tile([P, GROUPS, OUT], U8, align_bytes=64)
+        nc.vector.memset(w_scales[:].rearrange("p g n -> p (g n)").bitcast(I32), 0)
+        identity = keep.tile([P, P], F32)
+        make_identity(nc, identity[:])
+        ones = keep.tile([P, P], BF16)
+        nc.gpsimd.memset(ones[:], 1.0)
+
+        relations = {}
+        for t in range(TOKEN_TILES):
+            for q in range(QUARTERS):
+                token_major = keep.tile([P, QUARTER, CH], BF16, name="relations_%d_%d" % (t, q))
+                nc.sync.dma_start(
+                    out=token_major[:].rearrange("p j c -> p (j c)"),
+                    in_=x2[scenes(t), :, q * QUARTER : (q + 1) * QUARTER, :].rearrange("b i j c -> i b (j c)"),
+                )
+                relations[(t, q)] = token_major
+        plain = keep.tile([P, 2 * TOKEN_TILES, CH], BF16)
+        for t in range(TOKEN_TILES):
+            nc.sync.dma_start(
+                out=plain[:, t, :],
+                in_=x0[scenes(t), :].unsqueeze(0).to_broadcast([OBJECTS, TILE_SCENES, CH]),
+            )
+            nc.sync.dma_start(
+                out=plain[:, TOKEN_TILES + t, :], in_=x1[scenes(t), :, :].rearrange("b i c -> i b c")
+            )
+        for g0 in range(0, GROUPS, 2):
+            for first in range(2):
+                for r in range(4):
+                    nc.sync.dma_start(
+                        out=w_scales[32 * first + r : P : 64, g0 : g0 + 2, :].bitcast(I32),
+                        in_=W1_scales[g0 : g0 + 2, 4 * first + r : 16 : 8, :]
+                        .rearrange("g q n -> q g n")
+                        .bitcast(I32),
+                    )
+        w_words = keep.tile([P, GROUPS, 2 * OUT], U8, align_bytes=64)
+        for g in range(GROUPS):
+            nc.sync.dma_start(out=w_words[:, g, :].bitcast(I32), in_=W1_words[g].bitcast(I32))
+
+        turned = {}
+        for t in range(TOKEN_TILES):
+            for q in range(QUARTERS):
+                rows = keep.tile([P, QUARTER, CH], BF16, name="turned_%d_%d" % (t, q))
+                for s in range(0, QUARTER, BANK_ROWS):
+                    to_channel_major(
+                        nc, banks, identity[:], relations[(t, q)][:, s : s + BANK_ROWS, :], rows[:, s : s + BANK_ROWS, :]
+                    )
+                by_object = rows[:].bitcast(F32).rearrange("p s (i x) -> p (s i) x", x=OBJECT_WORDS)
+                step = OBJECTS + 1
+                for s, other in ((0, 2), (2, 0)):
+                    own = s * step + q * QUARTER
+                    lent = own + (other - s) * OBJECTS
+                    nc.scalar.copy(
+                        out=by_object[:, own : own + step + 1 : step, :],
+                        in_=by_object[:, lent : lent + step + 1 : step, :],
+                    )
+                turned[(t, q)] = rows
+
+        f1 = keep.tile([P, GROUPS * TOKEN_TILES, CH], BF16, align_bytes=64)
+        f1_words = keep.tile([P, GROUPS * TOKEN_TILES, P], U32, align_bytes=64)
+        f1_scales = keep.tile([P, GROUPS * TOKEN_TILES, P], U8, align_bytes=64)
+        for slot in range(0, 2 * TOKEN_TILES, BANK_ROWS):
+            to_channel_major(nc, banks, identity[:], plain[:, slot : slot + BANK_ROWS, :], f1[:, slot : slot + BANK_ROWS, :])
+
+        bias = keep.tile([P, OUT], F32)
+        for n in range(N_TILES):
+            cols = slice(n * N_TILE, (n + 1) * N_TILE)
+            spread = banks.tile([P, N_TILE], F32, tag="bank")
+            nc.tensor.matmul(spread[:], lhsT=ones[:], rhs=bias_row[:, cols], start=True, stop=True)
+            nc.scalar.copy(out=bias[:, cols], in_=spread[:])
+
+        def quantise(first, count):
+            slots = slice(first, first + count)
+            nc.vector.quantize_mx(
+                out=f1_words[:, slots, :].rearrange("p q m -> p (q m)").bitcast(FP8X4),
+                scales=f1_scales[:, slots, :].rearrange("p q m -> p (q m)"),
+                in_=f1[:, slots, :].rearrange("p q k -> p (q k)"),
+            )
+
+        pairs = {}
+
+        def reduce_quarters(t, quarters):
+            for q in quarters:
+                for kind, (op, fill) in enumerate(REDUCTIONS):
+                    pair = work.tile([P, 2, CH], BF16, tag="pair_%d" % kind)
+                    nc.vector.tensor_tensor(
+                        out=pair[:], in0=turned[(t, q)][:, 0:2, :], in1=turned[(t, q)][:, 2:4, :], op=op
+                    )
+                    pairs[(kind, q)] = pair
+                if q % 2 == 1:
+                    for kind, (op, fill) in enumerate(REDUCTIONS):
+                        joined = work.tile([P, 2, CH], BF16, tag="joined_%d" % kind)
+                        nc.vector.tensor_tensor(
+                            out=joined[:], in0=pairs[(kind, q - 1)][:], in1=pairs[(kind, q)][:], op=op
+                        )
+                        pairs[(kind, "joined", q // 2)] = joined
+
+        def close_reduction(t):
+            for kind, (op, fill) in enumerate(REDUCTIONS):
+                last = work.tile([P, 2, CH], BF16, tag="last_%d" % kind)
+                nc.vector.tensor_tensor(
+                    out=last[:], in0=pairs[(kind, "joined", 0)][:], in1=pairs[(kind, "joined", 1)][:], op=op
+                )
+                pairs[(kind, "last")] = last
+            for kind, (op, fill) in enumerate(REDUCTIONS):
+                last = pairs[(kind, "last")]
+                nc.vector.scalar_tensor_tensor(
+                    out=f1[:, (2 + kind) * TOKEN_TILES + t, :],
+                    in0=last[:, 0, :],
+                    scalar=fill,
+                    in1=last[:, 1, :],
+                    op0=op,
+                    op1=op,
+                )
+
+        sums = {}
+
+        def multiply(t, groups):
+            for g in groups:
+                slot = g * TOKEN_TILES + t
+                for n in range(N_TILES):
+                    if g == 0:
+                        bank = banks.tile([P, N_TILE], F32, tag="bank")
+                        sums[(t, n)] = bank
+                    nc.tensor.matmul_mx(
+                        out=sums[(t, n)][:],
+                        lhsT=f1_words[:, slot, :].bitcast(FP8X4),
+                        lhsT_scale=f1_scales[:, slot, :],
+                        rhs=w_words[:, g, 2 * n * N_TILE : 2 * (n + 1) * N_TILE].bitcast(FP4X4),
+                        rhs_scale=w_scales[:, g, n * N_TILE : (n + 1) * N_TILE],
+                        start=(g == 0),
+                        stop=(g == GROUPS - 1),
+                    )
+
+        def finish(t):
+            for n in range(N_TILES):
+                cols = slice(n * N_TILE, (n + 1) * N_TILE)
+                result = results.tile([P, N_TILE], F32)
+                nc.vector.tensor_tensor(out=result[:], in0=sums[(t, n)][:], in1=bias[:, cols], op=ALU.add)
+                nc.scalar.activation(out=result[:], in_=result[:], func=ACT.Sigmoid)
+                nc.sync.dma_start(out=out[scenes(t), :, cols].rearrange("b i o -> i b o"), in_=result[:])
+
+        reduce_quarters(0, range(QUARTERS))
+        close_reduction(0)
+        quantise(0, 2 * TOKEN_TILES)
+        quantise(2 * TOKEN_TILES, 1)
+        quantise(3 * TOKEN_TILES, 1)
+        multiply(0, range(GROUPS))
+        multiply(1, range(2))
+        reduce_quarters(1, range(QUARTERS - 1))
+        finish(0)
+        reduce_quarters(1, range(QUARTERS - 1, QUARTERS))
+        close_reduction(1)
+        quantise(2 * TOKEN_TILES + 1, 1)
+        multiply(1, range(2, 3))
+        quantise(3 * TOKEN_TILES + 1, 1)
+        multiply(1, range(3, 4))
+        finish(1)

@@ -70,7 +70,8 @@ def tile_differentiablelogicmachine_pb_kernel(tc, x0, x1, x2, W1_words, W1_scale
         nc.gpsimd.memset(ones[:], 1.0)
 
         relations = {}
-        for t in range(TOKEN_TILES):
+
+        def load_relations(t):
             for q in range(QUARTERS):
                 token_major = keep.tile([P, QUARTER, CH], BF16, name="relations_%d_%d" % (t, q))
                 nc.sync.dma_start(
@@ -78,6 +79,8 @@ def tile_differentiablelogicmachine_pb_kernel(tc, x0, x1, x2, W1_words, W1_scale
                     in_=x2[scenes(t), :, q * QUARTER : (q + 1) * QUARTER, :].rearrange("b i j c -> i b (j c)"),
                 )
                 relations[(t, q)] = token_major
+
+        load_relations(0)
         plain = keep.tile([P, 2 * TOKEN_TILES, CH], BF16)
         for t in range(TOKEN_TILES):
             nc.sync.dma_start(
@@ -87,6 +90,7 @@ def tile_differentiablelogicmachine_pb_kernel(tc, x0, x1, x2, W1_words, W1_scale
             nc.sync.dma_start(
                 out=plain[:, TOKEN_TILES + t, :], in_=x1[scenes(t), :, :].rearrange("b i c -> i b c")
             )
+        load_relations(1)
         for g0 in range(0, GROUPS, 2):
             for first in range(2):
                 for r in range(4):
@@ -101,7 +105,8 @@ def tile_differentiablelogicmachine_pb_kernel(tc, x0, x1, x2, W1_words, W1_scale
             nc.sync.dma_start(out=w_words[:, g, :].bitcast(I32), in_=W1_words[g].bitcast(I32))
 
         turned = {}
-        for t in range(TOKEN_TILES):
+
+        def turn_relations(t):
             for q in range(QUARTERS):
                 rows = keep.tile([P, QUARTER, CH], BF16, name="turned_%d_%d" % (t, q))
                 for s in range(0, QUARTER, BANK_ROWS):
@@ -122,8 +127,11 @@ def tile_differentiablelogicmachine_pb_kernel(tc, x0, x1, x2, W1_words, W1_scale
         f1 = keep.tile([P, GROUPS * TOKEN_TILES, CH], BF16, align_bytes=64)
         f1_words = keep.tile([P, GROUPS * TOKEN_TILES, P], U32, align_bytes=64)
         f1_scales = keep.tile([P, GROUPS * TOKEN_TILES, P], U8, align_bytes=64)
+
+        turn_relations(0)
         for slot in range(0, 2 * TOKEN_TILES, BANK_ROWS):
             to_channel_major(nc, banks, identity[:], plain[:, slot : slot + BANK_ROWS, :], f1[:, slot : slot + BANK_ROWS, :])
+        turn_relations(1)
 
         bias = keep.tile([P, OUT], F32)
         for n in range(N_TILES):

@@ -64,6 +64,8 @@ def tile_differentiablelogicmachine_pb_kernel(tc, x0, x1, x2, W1_words, W1_scale
         nc.scalar.dma_start(out=bias_row[0:1, :], in_=b1.rearrange("(o n) -> o n", o=1))
         w_scales = keep.tile([P, GROUPS, OUT], U8, align_bytes=64)
         nc.vector.memset(w_scales[:].rearrange("p g n -> p (g n)").bitcast(I32), 0)
+        nullary = keep.tile([P, CH], BF16)
+        nc.vector.memset(nullary[:].bitcast(I32), 0)
         identity = keep.tile([P, P], F32)
         make_identity(nc, identity[:])
         ones = keep.tile([P, P], BF16)
@@ -81,15 +83,10 @@ def tile_differentiablelogicmachine_pb_kernel(tc, x0, x1, x2, W1_words, W1_scale
                 relations[(t, q)] = token_major
 
         load_relations(0)
-        plain = keep.tile([P, 2 * TOKEN_TILES, CH], BF16)
+        nc.sync.dma_start(out=nullary[0:SCENES, :], in_=x0)
+        unary = keep.tile([P, TOKEN_TILES, CH], BF16)
         for t in range(TOKEN_TILES):
-            nc.sync.dma_start(
-                out=plain[:, t, :],
-                in_=x0[scenes(t), :].unsqueeze(0).to_broadcast([OBJECTS, TILE_SCENES, CH]),
-            )
-            nc.sync.dma_start(
-                out=plain[:, TOKEN_TILES + t, :], in_=x1[scenes(t), :, :].rearrange("b i c -> i b c")
-            )
+            nc.sync.dma_start(out=unary[:, t, :], in_=x1[scenes(t), :, :].rearrange("b i c -> i b c"))
         load_relations(1)
         for g0 in range(0, GROUPS, 2):
             for first in range(2):
@@ -129,8 +126,18 @@ def tile_differentiablelogicmachine_pb_kernel(tc, x0, x1, x2, W1_words, W1_scale
         f1_scales = keep.tile([P, GROUPS * TOKEN_TILES, P], U8, align_bytes=64)
 
         turn_relations(0)
-        for slot in range(0, 2 * TOKEN_TILES, BANK_ROWS):
-            to_channel_major(nc, banks, identity[:], plain[:, slot : slot + BANK_ROWS, :], f1[:, slot : slot + BANK_ROWS, :])
+        scene_words = banks.tile([P, WORD_HALVES, P], F32, tag="bank")
+        for u in range(WORD_HALVES):
+            nc.tensor.transpose(scene_words[:, u, :], nullary[:].bitcast(F32)[:, u : CH // 2 : WORD_HALVES], identity[:])
+        for t in range(TOKEN_TILES):
+            nc.scalar.copy(
+                out=f1[:, t, :].bitcast(F32).rearrange("p (i b u) -> p i b u", i=OBJECTS, u=WORD_HALVES),
+                in_=scene_words[:, :, scenes(t)]
+                .rearrange("p u b -> p b u")
+                .unsqueeze(1)
+                .to_broadcast([P, OBJECTS, TILE_SCENES, WORD_HALVES]),
+            )
+        to_channel_major(nc, banks, identity[:], unary[:], f1[:, TOKEN_TILES : 2 * TOKEN_TILES, :])
         turn_relations(1)
 
         bias = keep.tile([P, OUT], F32)

@@ -88,15 +88,11 @@ def tile_differentiablelogicmachine_pb_kernel(tc, x0, x1, x2, W1_words, W1_scale
         for t in range(TOKEN_TILES):
             nc.sync.dma_start(out=unary[:, t, :], in_=x1[scenes(t), :, :].rearrange("b i c -> i b c"))
         load_relations(1)
-        for g0 in range(0, GROUPS, 2):
-            for first in range(2):
-                for r in range(4):
-                    nc.sync.dma_start(
-                        out=w_scales[32 * first + r : P : 64, g0 : g0 + 2, :].bitcast(I32),
-                        in_=W1_scales[g0 : g0 + 2, 4 * first + r : 16 : 8, :]
-                        .rearrange("g q n -> q g n")
-                        .bitcast(I32),
-                    )
+        for r in range(4):
+            nc.sync.dma_start(
+                out=w_scales[r:P:32, :, :].bitcast(I32),
+                in_=W1_scales[:, r:16:4, :].rearrange("g q n -> q g n").bitcast(I32),
+            )
         w_words = keep.tile([P, GROUPS, 2 * OUT], U8, align_bytes=64)
         for g in range(GROUPS):
             nc.sync.dma_start(out=w_words[:, g, :].bitcast(I32), in_=W1_words[g].bitcast(I32))

@@ -28,19 +28,21 @@ QUARTERS = OBJECTS // QUARTER
 BANK_ROWS = 2
 N_TILE = 512
 N_TILES = OUT // N_TILE
-OBJECT_WORDS = TILE_SCENES * WORD_HALVES
+OBJECT_RUN = TILE_SCENES * PACK
 
 FLOPS = 2 * SCENES * OBJECTS * GROUPS * CH * OUT
 
-REDUCTIONS = ((ALU.max, 0.0), (ALU.min, 1.0))
+MAX = 0
+MIN = 1
+OPS = (ALU.max, ALU.min)
 
 
-def to_channel_major(nc, banks, identity, src, dst):
+def to_channel_major(nc, banks, selectors, src, dst):
     words = banks.tile([P, BANK_ROWS, WORD_HALVES, P], F32, tag="bank")
     for s in range(BANK_ROWS):
         src_words = src[:, s, :].bitcast(F32)
         for u in range(WORD_HALVES):
-            nc.tensor.transpose(words[:, s, u, :], src_words[:, u : CH // 2 : WORD_HALVES], identity)
+            nc.tensor.transpose(words[:, s, u, :], src_words[:, u : CH // 2 : WORD_HALVES], selectors[s])
     nc.scalar.copy(
         out=dst.bitcast(F32).rearrange("p s (k u) -> p s k u", u=WORD_HALVES),
         in_=words[:].rearrange("p s u k -> p s k u"),
@@ -70,6 +72,11 @@ def tile_differentiablelogicmachine_pb_kernel(tc, x0, x1, x2, W1_words, W1_scale
         make_identity(nc, identity[:])
         ones = keep.tile([P, P], BF16)
         nc.gpsimd.memset(ones[:], 1.0)
+        without = keep.tile([P, OBJECTS, P], F32)
+        nc.vector.tensor_copy(out=without[:], in_=identity[:].unsqueeze(1).to_broadcast([P, OBJECTS, P]))
+        nc.vector.memset(
+            without[:].rearrange("p j (i b) -> p (j i) b", b=TILE_SCENES)[:, 0 : OBJECTS * OBJECTS : OBJECTS + 1, :], 0.0
+        )
 
         relations = {}
 
@@ -103,17 +110,13 @@ def tile_differentiablelogicmachine_pb_kernel(tc, x0, x1, x2, W1_words, W1_scale
             for q in range(QUARTERS):
                 rows = keep.tile([P, QUARTER, CH], BF16, name="turned_%d_%d" % (t, q))
                 for s in range(0, QUARTER, BANK_ROWS):
+                    j = q * QUARTER + s
                     to_channel_major(
-                        nc, banks, identity[:], relations[(t, q)][:, s : s + BANK_ROWS, :], rows[:, s : s + BANK_ROWS, :]
-                    )
-                by_object = rows[:].bitcast(F32).rearrange("p s (i x) -> p (s i) x", x=OBJECT_WORDS)
-                step = OBJECTS + 1
-                for s, other in ((0, 2), (2, 0)):
-                    own = s * step + q * QUARTER
-                    lent = own + (other - s) * OBJECTS
-                    nc.scalar.copy(
-                        out=by_object[:, own : own + step + 1 : step, :],
-                        in_=by_object[:, lent : lent + step + 1 : step, :],
+                        nc,
+                        banks,
+                        [without[:, j + k, :] for k in range(BANK_ROWS)],
+                        relations[(t, q)][:, s : s + BANK_ROWS, :],
+                        rows[:, s : s + BANK_ROWS, :],
                     )
                 turned[(t, q)] = rows
 
@@ -133,7 +136,7 @@ def tile_differentiablelogicmachine_pb_kernel(tc, x0, x1, x2, W1_words, W1_scale
                 .unsqueeze(1)
                 .to_broadcast([P, OBJECTS, TILE_SCENES, WORD_HALVES]),
             )
-        to_channel_major(nc, banks, identity[:], unary[:], f1[:, TOKEN_TILES : 2 * TOKEN_TILES, :])
+        to_channel_major(nc, banks, [identity[:]] * BANK_ROWS, unary[:], f1[:, TOKEN_TILES : 2 * TOKEN_TILES, :])
         turn_relations(1)
 
         bias = keep.tile([P, OUT], F32)
@@ -151,41 +154,43 @@ def tile_differentiablelogicmachine_pb_kernel(tc, x0, x1, x2, W1_words, W1_scale
                 in_=f1[:, slots, :].rearrange("p q k -> p (q k)"),
             )
 
-        pairs = {}
+        def halve(t, q, kind):
+            pair = work.tile([P, 2, CH], BF16, tag="pair_%d" % kind)
+            rows = turned[(t, q)]
+            nc.vector.tensor_tensor(out=pair[:], in0=rows[:, 0:2, :], in1=rows[:, 2:4, :], op=OPS[kind])
+            return pair
 
-        def reduce_quarters(t, quarters):
-            for q in quarters:
-                for kind, (op, fill) in enumerate(REDUCTIONS):
-                    pair = work.tile([P, 2, CH], BF16, tag="pair_%d" % kind)
-                    nc.vector.tensor_tensor(
-                        out=pair[:], in0=turned[(t, q)][:, 0:2, :], in1=turned[(t, q)][:, 2:4, :], op=op
-                    )
-                    pairs[(kind, q)] = pair
-                if q % 2 == 1:
-                    for kind, (op, fill) in enumerate(REDUCTIONS):
-                        joined = work.tile([P, 2, CH], BF16, tag="joined_%d" % kind)
-                        nc.vector.tensor_tensor(
-                            out=joined[:], in0=pairs[(kind, q - 1)][:], in1=pairs[(kind, q)][:], op=op
-                        )
-                        pairs[(kind, "joined", q // 2)] = joined
+        def join(kind, best, pair):
+            joined = work.tile([P, 2, CH], BF16, tag="best_%d" % kind)
+            nc.vector.tensor_tensor(out=joined[:], in0=best[:], in1=pair[:], op=OPS[kind])
+            return joined
 
-        def close_reduction(t):
-            for kind, (op, fill) in enumerate(REDUCTIONS):
-                last = work.tile([P, 2, CH], BF16, tag="last_%d" % kind)
-                nc.vector.tensor_tensor(
-                    out=last[:], in0=pairs[(kind, "joined", 0)][:], in1=pairs[(kind, "joined", 1)][:], op=op
-                )
-                pairs[(kind, "last")] = last
-            for kind, (op, fill) in enumerate(REDUCTIONS):
-                last = pairs[(kind, "last")]
-                nc.vector.scalar_tensor_tensor(
-                    out=f1[:, (2 + kind) * TOKEN_TILES + t, :],
-                    in0=last[:, 0, :],
-                    scalar=fill,
-                    in1=last[:, 1, :],
-                    op0=op,
-                    op1=op,
-                )
+        def refill(t, q):
+            by_object = turned[(t, q)][:].rearrange("p s (i x) -> p (s i) x", x=OBJECT_RUN)
+            first = q * QUARTER
+            nc.vector.memset(by_object[:, first : first + (OBJECTS + 1) * (QUARTER - 1) + 1 : OBJECTS + 1, :], 1.0)
+
+        def last_step(t, kind, best):
+            nc.vector.tensor_tensor(
+                out=f1[:, (2 + kind) * TOKEN_TILES + t, :], in0=best[:, 0, :], in1=best[:, 1, :], op=OPS[kind]
+            )
+
+        def reduce_tile(t, between):
+            for q in range(QUARTERS):
+                high = halve(t, q, MAX)
+                if q == 1:
+                    low_best = low
+                if q > 1:
+                    low_best = join(MIN, low_best, low)
+                refill(t, q)
+                high_best = high if q == 0 else join(MAX, high_best, high)
+                low = halve(t, q, MIN)
+                if q == QUARTERS - 2:
+                    between()
+            last_step(t, MAX, high_best)
+            low_best = join(MIN, low_best, low)
+            quantise(2 * TOKEN_TILES + t, 1)
+            last_step(t, MIN, low_best)
 
         sums = {}
 
@@ -214,18 +219,15 @@ def tile_differentiablelogicmachine_pb_kernel(tc, x0, x1, x2, W1_words, W1_scale
                 nc.scalar.activation(out=result[:], in_=result[:], func=ACT.Sigmoid)
                 nc.sync.dma_start(out=out[scenes(t), :, cols].rearrange("b i o -> i b o"), in_=result[:])
 
-        reduce_quarters(0, range(QUARTERS))
-        close_reduction(0)
+        def nothing():
+            return None
+
+        reduce_tile(0, nothing)
         quantise(0, 2 * TOKEN_TILES)
-        quantise(2 * TOKEN_TILES, 1)
         quantise(3 * TOKEN_TILES, 1)
         multiply(0, range(GROUPS))
         multiply(1, range(2))
-        reduce_quarters(1, range(QUARTERS - 1))
-        finish(0)
-        reduce_quarters(1, range(QUARTERS - 1, QUARTERS))
-        close_reduction(1)
-        quantise(2 * TOKEN_TILES + 1, 1)
+        reduce_tile(1, lambda: finish(0))
         multiply(1, range(2, 3))
         quantise(3 * TOKEN_TILES + 1, 1)
         multiply(1, range(3, 4))

@@ -29,6 +29,7 @@ BANK_ROWS = 2
 N_TILE = 512
 N_TILES = OUT // N_TILE
 OBJECT_RUN = TILE_SCENES * PACK
+DIAGONAL = OBJECTS + 1
 
 FLOPS = 2 * SCENES * OBJECTS * GROUPS * CH * OUT
 
@@ -54,29 +55,33 @@ def tile_differentiablelogicmachine_pb_kernel(tc, x0, x1, x2, W1_words, W1_scale
     with ExitStack() as stack:
         keep = stack.enter_context(tc.tile_pool(name="keep", bufs=1))
         work = stack.enter_context(tc.tile_pool(name="work", bufs=2))
-        results = stack.enter_context(tc.tile_pool(name="results", bufs=4))
-        banks = stack.enter_context(tc.psum_pool(name="banks", bufs=8))
+        results = stack.enter_context(tc.tile_pool(name="results", bufs=TOKEN_TILES * N_TILES))
+        banks = stack.enter_context(tc.psum_pool(name="banks", bufs=4))
+        sums_0 = stack.enter_context(tc.psum_pool(name="sums_0", bufs=4))
         stack.enter_context(tc.manual_schedule())
 
         def scenes(t):
             return slice(t * TILE_SCENES, (t + 1) * TILE_SCENES)
 
-        bias_row = keep.tile([P, OUT], BF16)
-        nc.vector.memset(bias_row[:].bitcast(I32), 0)
-        nc.scalar.dma_start(out=bias_row[0:1, :], in_=b1.rearrange("(o n) -> o n", o=1))
-        w_scales = keep.tile([P, GROUPS, OUT], U8, align_bytes=64)
-        nc.vector.memset(w_scales[:].rearrange("p g n -> p (g n)").bitcast(I32), 0)
-        nullary = keep.tile([P, CH], BF16)
-        nc.vector.memset(nullary[:].bitcast(I32), 0)
         identity = keep.tile([P, P], F32)
         make_identity(nc, identity[:])
-        ones = keep.tile([P, P], BF16)
-        nc.gpsimd.memset(ones[:], 1.0)
+        nullary = keep.tile([P, CH], BF16)
+        nc.vector.memset(nullary[:].bitcast(I32), 0)
+        table_loaded = keep.tile([P, 1], F32)
+        nc.scalar.activation(out=table_loaded[:], in_=nullary[:, 0:1], func=ACT.Sigmoid)
+        w_scales = keep.tile([P, GROUPS, OUT], U8, align_bytes=64)
+        nc.vector.memset(w_scales[:].rearrange("p g n -> p (g n)").bitcast(I32), 0)
         without = keep.tile([P, OBJECTS, P], F32)
-        nc.vector.tensor_copy(out=without[:], in_=identity[:].unsqueeze(1).to_broadcast([P, OBJECTS, P]))
-        nc.vector.memset(
-            without[:].rearrange("p j (i b) -> p (j i) b", b=TILE_SCENES)[:, 0 : OBJECTS * OBJECTS : OBJECTS + 1, :], 0.0
-        )
+        for q in range(QUARTERS):
+            four = without[:, q * QUARTER : (q + 1) * QUARTER, :]
+            nc.vector.tensor_copy(out=four, in_=identity[:].unsqueeze(1).to_broadcast([P, QUARTER, P]))
+            first = q * QUARTER
+            nc.vector.memset(
+                four.rearrange("p j (i b) -> p (j i) b", b=TILE_SCENES)[
+                    :, first : first + DIAGONAL * (QUARTER - 1) + 1 : DIAGONAL, :
+                ],
+                0.0,
+            )
 
         relations = {}
 
@@ -103,6 +108,8 @@ def tile_differentiablelogicmachine_pb_kernel(tc, x0, x1, x2, W1_words, W1_scale
         w_words = keep.tile([P, GROUPS, 2 * OUT], U8, align_bytes=64)
         for g in range(GROUPS):
             nc.sync.dma_start(out=w_words[:, g, :].bitcast(I32), in_=W1_words[g].bitcast(I32))
+        bias = keep.tile([P, OUT], BF16)
+        nc.sync.dma_start(out=bias[:], in_=b1.partition_broadcast(P))
 
         turned = {}
 
@@ -139,13 +146,6 @@ def tile_differentiablelogicmachine_pb_kernel(tc, x0, x1, x2, W1_words, W1_scale
         to_channel_major(nc, banks, [identity[:]] * BANK_ROWS, unary[:], f1[:, TOKEN_TILES : 2 * TOKEN_TILES, :])
         turn_relations(1)
 
-        bias = keep.tile([P, OUT], F32)
-        for n in range(N_TILES):
-            cols = slice(n * N_TILE, (n + 1) * N_TILE)
-            spread = banks.tile([P, N_TILE], F32, tag="bank")
-            nc.tensor.matmul(spread[:], lhsT=ones[:], rhs=bias_row[:, cols], start=True, stop=True)
-            nc.scalar.copy(out=bias[:, cols], in_=spread[:])
-
         def quantise(first, count):
             slots = slice(first, first + count)
             nc.vector.quantize_mx(
@@ -168,14 +168,14 @@ def tile_differentiablelogicmachine_pb_kernel(tc, x0, x1, x2, W1_words, W1_scale
         def refill(t, q):
             by_object = turned[(t, q)][:].rearrange("p s (i x) -> p (s i) x", x=OBJECT_RUN)
             first = q * QUARTER
-            nc.vector.memset(by_object[:, first : first + (OBJECTS + 1) * (QUARTER - 1) + 1 : OBJECTS + 1, :], 1.0)
+            nc.vector.memset(by_object[:, first : first + DIAGONAL * (QUARTER - 1) + 1 : DIAGONAL, :], 1.0)
 
         def last_step(t, kind, best):
             nc.vector.tensor_tensor(
                 out=f1[:, (2 + kind) * TOKEN_TILES + t, :], in0=best[:, 0, :], in1=best[:, 1, :], op=OPS[kind]
             )
 
-        def reduce_tile(t, between):
+        def reduce_tile(t):
             for q in range(QUARTERS):
                 high = halve(t, q, MAX)
                 if q == 1:
@@ -185,8 +185,6 @@ def tile_differentiablelogicmachine_pb_kernel(tc, x0, x1, x2, W1_words, W1_scale
                 refill(t, q)
                 high_best = high if q == 0 else join(MAX, high_best, high)
                 low = halve(t, q, MIN)
-                if q == QUARTERS - 2:
-                    between()
             last_step(t, MAX, high_best)
             low_best = join(MIN, low_best, low)
             quantise(2 * TOKEN_TILES + t, 1)
@@ -194,22 +192,21 @@ def tile_differentiablelogicmachine_pb_kernel(tc, x0, x1, x2, W1_words, W1_scale
 
         sums = {}
 
-        def multiply(t, groups):
-            for g in groups:
-                slot = g * TOKEN_TILES + t
-                for n in range(N_TILES):
-                    if g == 0:
-                        bank = banks.tile([P, N_TILE], F32, tag="bank")
-                        sums[(t, n)] = bank
-                    nc.tensor.matmul_mx(
-                        out=sums[(t, n)][:],
-                        lhsT=f1_words[:, slot, :].bitcast(FP8X4),
-                        lhsT_scale=f1_scales[:, slot, :],
-                        rhs=w_words[:, g, 2 * n * N_TILE : 2 * (n + 1) * N_TILE].bitcast(FP4X4),
-                        rhs_scale=w_scales[:, g, n * N_TILE : (n + 1) * N_TILE],
-                        start=(g == 0),
-                        stop=(g == GROUPS - 1),
-                    )
+        def one_pass(t, g, n):
+            if g == 0:
+                pool = sums_0 if t == 0 else banks
+                bank = pool.tile([P, N_TILE], F32, tag="bank")
+                sums[(t, n)] = bank
+            slot = g * TOKEN_TILES + t
+            nc.tensor.matmul_mx(
+                out=sums[(t, n)][:],
+                lhsT=f1_words[:, slot, :].bitcast(FP8X4),
+                lhsT_scale=f1_scales[:, slot, :],
+                rhs=w_words[:, g, 2 * n * N_TILE : 2 * (n + 1) * N_TILE].bitcast(FP4X4),
+                rhs_scale=w_scales[:, g, n * N_TILE : (n + 1) * N_TILE],
+                start=(g == 0),
+                stop=(g == GROUPS - 1),
+            )
 
         def finish(t):
             for n in range(N_TILES):
@@ -219,16 +216,19 @@ def tile_differentiablelogicmachine_pb_kernel(tc, x0, x1, x2, W1_words, W1_scale
                 nc.scalar.activation(out=result[:], in_=result[:], func=ACT.Sigmoid)
                 nc.sync.dma_start(out=out[scenes(t), :, cols].rearrange("b i o -> i b o"), in_=result[:])
 
-        def nothing():
-            return None
-
-        reduce_tile(0, nothing)
+        reduce_tile(0)
         quantise(0, 2 * TOKEN_TILES)
         quantise(3 * TOKEN_TILES, 1)
-        multiply(0, range(GROUPS))
-        multiply(1, range(2))
-        reduce_tile(1, lambda: finish(0))
-        multiply(1, range(2, 3))
+        for g in range(GROUPS):
+            for n in range(N_TILES):
+                one_pass(0, g, n)
+        for g in range(2):
+            for n in range(N_TILES):
+                one_pass(1, g, n)
+        reduce_tile(1)
         quantise(3 * TOKEN_TILES + 1, 1)
-        multiply(1, range(3, 4))
+        for n in range(N_TILES):
+            for g in range(2, GROUPS):
+                one_pass(1, g, n)
+        finish(0)
         finish(1)

@@ -86,13 +86,13 @@ def tile_differentiablelogicmachine_pb_kernel(tc, x0, x1, x2, W1_words, W1_scale
         relations = {}
 
         def load_relations(t):
-            for q in range(QUARTERS):
-                token_major = keep.tile([P, QUARTER, CH], BF16, name="relations_%d_%d" % (t, q))
+            for j in range(0, OBJECTS, BANK_ROWS):
+                token_major = keep.tile([P, BANK_ROWS, CH], BF16, name="relations_%d_%d" % (t, j))
                 nc.sync.dma_start(
                     out=token_major[:].rearrange("p j c -> p (j c)"),
-                    in_=x2[scenes(t), :, q * QUARTER : (q + 1) * QUARTER, :].rearrange("b i j c -> i b (j c)"),
+                    in_=x2[scenes(t), :, j : j + BANK_ROWS, :].rearrange("b i j c -> i b (j c)"),
                 )
-                relations[(t, q)] = token_major
+                relations[(t, j)] = token_major
 
         load_relations(0)
         nc.sync.dma_start(out=nullary[0:SCENES, :], in_=x0)
@@ -122,7 +122,7 @@ def tile_differentiablelogicmachine_pb_kernel(tc, x0, x1, x2, W1_words, W1_scale
                         nc,
                         banks,
                         [without[:, j + k, :] for k in range(BANK_ROWS)],
-                        relations[(t, q)][:, s : s + BANK_ROWS, :],
+                        relations[(t, j)][:],
                         rows[:, s : s + BANK_ROWS, :],
                     )
                 turned[(t, q)] = rows
@@ -175,7 +175,7 @@ def tile_differentiablelogicmachine_pb_kernel(tc, x0, x1, x2, W1_words, W1_scale
                 out=f1[:, (2 + kind) * TOKEN_TILES + t, :], in0=best[:, 0, :], in1=best[:, 1, :], op=OPS[kind]
             )
 
-        def reduce_tile(t):
+        def reduce_tile(t, meanwhile):
             for q in range(QUARTERS):
                 high = halve(t, q, MAX)
                 if q == 1:
@@ -188,7 +188,9 @@ def tile_differentiablelogicmachine_pb_kernel(tc, x0, x1, x2, W1_words, W1_scale
             last_step(t, MAX, high_best)
             low_best = join(MIN, low_best, low)
             quantise(2 * TOKEN_TILES + t, 1)
+            meanwhile()
             last_step(t, MIN, low_best)
+            quantise(3 * TOKEN_TILES + t, 1)
 
         sums = {}
 
@@ -208,27 +210,24 @@ def tile_differentiablelogicmachine_pb_kernel(tc, x0, x1, x2, W1_words, W1_scale
                 stop=(g == GROUPS - 1),
             )
 
-        def finish(t):
-            for n in range(N_TILES):
+        def finish(t, some_banks):
+            for n in some_banks:
                 cols = slice(n * N_TILE, (n + 1) * N_TILE)
                 result = results.tile([P, N_TILE], F32)
                 nc.vector.tensor_tensor(out=result[:], in0=sums[(t, n)][:], in1=bias[:, cols], op=ALU.add)
                 nc.scalar.activation(out=result[:], in_=result[:], func=ACT.Sigmoid)
                 nc.sync.dma_start(out=out[scenes(t), :, cols].rearrange("b i o -> i b o"), in_=result[:])
 
-        reduce_tile(0)
-        quantise(0, 2 * TOKEN_TILES)
-        quantise(3 * TOKEN_TILES, 1)
-        for g in range(GROUPS):
-            for n in range(N_TILES):
+        reduce_tile(0, lambda: quantise(0, 2 * TOKEN_TILES))
+        for n in range(N_TILES):
+            for g in range(GROUPS):
                 one_pass(0, g, n)
         for g in range(2):
             for n in range(N_TILES):
                 one_pass(1, g, n)
-        reduce_tile(1)
-        quantise(3 * TOKEN_TILES + 1, 1)
-        for n in range(N_TILES):
-            for g in range(2, GROUPS):
+        reduce_tile(1, lambda: finish(0, range(N_TILES // 2)))
+        for g in range(2, GROUPS):
+            for n in range(N_TILES):
                 one_pass(1, g, n)
-        finish(0)
-        finish(1)
+        finish(0, range(N_TILES // 2, N_TILES))
+        finish(1, range(N_TILES))

@@ -28,8 +28,6 @@ QUARTERS = OBJECTS // QUARTER
 BANK_ROWS = 2
 N_TILE = 512
 N_TILES = OUT // N_TILE
-OBJECT_RUN = TILE_SCENES * PACK
-DIAGONAL = OBJECTS + 1
 
 FLOPS = 2 * SCENES * OBJECTS * GROUPS * CH * OUT
 
@@ -48,6 +46,11 @@ def to_channel_major(nc, banks, selectors, src, dst):
         out=dst.bitcast(F32).rearrange("p s (k u) -> p s k u", u=WORD_HALVES),
         in_=words[:].rearrange("p s u k -> p s k u"),
     )
+
+
+def diagonal(flat, row, run):
+    rows = flat[:, 0 : OBJECTS * (row + run)].rearrange("p (j k) -> p j k", k=row + run)
+    return rows[:, :, 0:row].rearrange("p j (b k) -> p j b k", b=TILE_SCENES)[:, :, :, 0:run]
 
 
 def tile_differentiablelogicmachine_pb_kernel(tc, x0, x1, x2, W1_words, W1_scales, b1, out):
@@ -71,17 +74,13 @@ def tile_differentiablelogicmachine_pb_kernel(tc, x0, x1, x2, W1_words, W1_scale
         nc.scalar.activation(out=table_loaded[:], in_=nullary[:, 0:1], func=ACT.Sigmoid)
         w_scales = keep.tile([P, GROUPS, OUT], U8, align_bytes=64)
         nc.vector.memset(w_scales[:].rearrange("p g n -> p (g n)").bitcast(I32), 0)
-        without = keep.tile([P, OBJECTS, P], F32)
+        without_flat = keep.tile([P, OBJECTS * (P + 1)], F32)
+        without = without_flat[:, 0 : OBJECTS * P].rearrange("p (j k) -> p j k", k=P)
         for q in range(QUARTERS):
             four = without[:, q * QUARTER : (q + 1) * QUARTER, :]
             nc.vector.tensor_copy(out=four, in_=identity[:].unsqueeze(1).to_broadcast([P, QUARTER, P]))
             first = q * QUARTER
-            nc.vector.memset(
-                four.rearrange("p j (i b) -> p (j i) b", b=TILE_SCENES)[
-                    :, first : first + DIAGONAL * (QUARTER - 1) + 1 : DIAGONAL, :
-                ],
-                0.0,
-            )
+            nc.vector.memset(diagonal(without_flat, P, 1)[:, first : first + QUARTER, :, :], 0.0)
 
         relations = {}
 
@@ -90,7 +89,7 @@ def tile_differentiablelogicmachine_pb_kernel(tc, x0, x1, x2, W1_words, W1_scale
                 token_major = keep.tile([P, BANK_ROWS, CH], BF16, name="relations_%d_%d" % (t, j))
                 nc.sync.dma_start(
                     out=token_major[:].rearrange("p j c -> p (j c)"),
-                    in_=x2[scenes(t), :, j : j + BANK_ROWS, :].rearrange("b i j c -> i b (j c)"),
+                    in_=x2[scenes(t), :, j : j + BANK_ROWS, :].rearrange("b i j c -> (b i) (j c)"),
                 )
                 relations[(t, j)] = token_major
 
@@ -98,7 +97,7 @@ def tile_differentiablelogicmachine_pb_kernel(tc, x0, x1, x2, W1_words, W1_scale
         nc.sync.dma_start(out=nullary[0:SCENES, :], in_=x0)
         unary = keep.tile([P, TOKEN_TILES, CH], BF16)
         for t in range(TOKEN_TILES):
-            nc.sync.dma_start(out=unary[:, t, :], in_=x1[scenes(t), :, :].rearrange("b i c -> i b c"))
+            nc.sync.dma_start(out=unary[:, t, :], in_=x1[scenes(t), :, :].rearrange("b i c -> (b i) c"))
         load_relations(1)
         for r in range(4):
             nc.sync.dma_start(
@@ -112,10 +111,12 @@ def tile_differentiablelogicmachine_pb_kernel(tc, x0, x1, x2, W1_words, W1_scale
         nc.sync.dma_start(out=bias[:], in_=b1.partition_broadcast(P))
 
         turned = {}
+        turned_flat = [keep.tile([P, OBJECTS * (CH + PACK)], BF16, name="turned_%d" % t) for t in range(TOKEN_TILES)]
 
         def turn_relations(t):
             for q in range(QUARTERS):
-                rows = keep.tile([P, QUARTER, CH], BF16, name="turned_%d_%d" % (t, q))
+                first = q * QUARTER
+                rows = turned_flat[t][:, first * CH : (first + QUARTER) * CH].rearrange("p (s k) -> p s k", k=CH)
                 for s in range(0, QUARTER, BANK_ROWS):
                     j = q * QUARTER + s
                     to_channel_major(
@@ -137,11 +138,11 @@ def tile_differentiablelogicmachine_pb_kernel(tc, x0, x1, x2, W1_words, W1_scale
             nc.tensor.transpose(scene_words[:, u, :], nullary[:].bitcast(F32)[:, u : CH // 2 : WORD_HALVES], identity[:])
         for t in range(TOKEN_TILES):
             nc.scalar.copy(
-                out=f1[:, t, :].bitcast(F32).rearrange("p (i b u) -> p i b u", i=OBJECTS, u=WORD_HALVES),
+                out=f1[:, t, :].bitcast(F32).rearrange("p (b i u) -> p b i u", i=OBJECTS, u=WORD_HALVES),
                 in_=scene_words[:, :, scenes(t)]
                 .rearrange("p u b -> p b u")
-                .unsqueeze(1)
-                .to_broadcast([P, OBJECTS, TILE_SCENES, WORD_HALVES]),
+                .unsqueeze(2)
+                .to_broadcast([P, TILE_SCENES, OBJECTS, WORD_HALVES]),
             )
         to_channel_major(nc, banks, [identity[:]] * BANK_ROWS, unary[:], f1[:, TOKEN_TILES : 2 * TOKEN_TILES, :])
         turn_relations(1)
@@ -166,9 +167,8 @@ def tile_differentiablelogicmachine_pb_kernel(tc, x0, x1, x2, W1_words, W1_scale
             return joined
 
         def refill(t, q):
-            by_object = turned[(t, q)][:].rearrange("p s (i x) -> p (s i) x", x=OBJECT_RUN)
             first = q * QUARTER
-            nc.vector.memset(by_object[:, first : first + DIAGONAL * (QUARTER - 1) + 1 : DIAGONAL, :], 1.0)
+            nc.vector.memset(diagonal(turned_flat[t], CH, PACK)[:, first : first + QUARTER, :, :], 1.0)
 
         def last_step(t, kind, best):
             nc.vector.tensor_tensor(
@@ -216,7 +216,7 @@ def tile_differentiablelogicmachine_pb_kernel(tc, x0, x1, x2, W1_words, W1_scale
                 result = results.tile([P, N_TILE], F32)
                 nc.vector.tensor_tensor(out=result[:], in0=sums[(t, n)][:], in1=bias[:, cols], op=ALU.add)
                 nc.scalar.activation(out=result[:], in_=result[:], func=ACT.Sigmoid)
-                nc.sync.dma_start(out=out[scenes(t), :, cols].rearrange("b i o -> i b o"), in_=result[:])
+                nc.sync.dma_start(out=out[scenes(t), :, cols].rearrange("b i o -> (b i) o"), in_=result[:])
 
         reduce_tile(0, lambda: quantise(0, 2 * TOKEN_TILES))
         for n in range(N_TILES):

@@ -21,50 +21,46 @@ OUT = 2048
 PACK = 4
 WORD_HALVES = 2
 GROUPS = 4
-TILE_SCENES = P // OBJECTS
-TOKEN_TILES = SCENES // TILE_SCENES
-QUARTER = 4
-QUARTERS = OBJECTS // QUARTER
+TOKEN_TILES = 2
+TILE_OBJECTS = P // SCENES
+CHUNK = 4
+CHUNKS = OBJECTS // CHUNK
 BANK_ROWS = 2
 N_TILE = 512
 N_TILES = OUT // N_TILE
+FLIPPED = 2
+EARLY = 2
+SLOTS = 7
 
 FLOPS = 2 * SCENES * OBJECTS * GROUPS * CH * OUT
 
 MAX = 0
 MIN = 1
+KINDS = (MAX, MIN)
 OPS = (ALU.max, ALU.min)
 
 
-def to_channel_major(nc, banks, selectors, src, dst):
-    words = banks.tile([P, BANK_ROWS, WORD_HALVES, P], F32, tag="bank")
-    for s in range(BANK_ROWS):
-        src_words = src[:, s, :].bitcast(F32)
-        for u in range(WORD_HALVES):
-            nc.tensor.transpose(words[:, s, u, :], src_words[:, u : CH // 2 : WORD_HALVES], selectors[s])
-    nc.scalar.copy(
-        out=dst.bitcast(F32).rearrange("p s (k u) -> p s k u", u=WORD_HALVES),
-        in_=words[:].rearrange("p s u k -> p s k u"),
-    )
+def f1_slot(g, t):
+    return (0, 1 + t, 3 + 2 * t, 4 + 2 * t)[g]
 
 
 def diagonal(flat, row, run):
-    rows = flat[:, 0 : OBJECTS * (row + run)].rearrange("p (j k) -> p j k", k=row + run)
-    return rows[:, :, 0:row].rearrange("p j (b k) -> p j b k", b=TILE_SCENES)[:, :, :, 0:run]
+    rows = flat[:, 0 : TILE_OBJECTS * (row + run)].rearrange("p (s k) -> p s k", k=row + run)
+    return rows[:, :, 0:row].rearrange("p s (b k) -> p s b k", b=SCENES)[:, :, :, 0:run]
 
 
 def tile_differentiablelogicmachine_pb_kernel(tc, x0, x1, x2, W1_words, W1_scales, b1, out):
     nc = tc.nc
     with ExitStack() as stack:
         keep = stack.enter_context(tc.tile_pool(name="keep", bufs=1))
-        work = stack.enter_context(tc.tile_pool(name="work", bufs=2))
-        results = stack.enter_context(tc.tile_pool(name="results", bufs=TOKEN_TILES * N_TILES))
-        banks = stack.enter_context(tc.psum_pool(name="banks", bufs=4))
-        sums_0 = stack.enter_context(tc.psum_pool(name="sums_0", bufs=4))
+        banks = stack.enter_context(tc.psum_pool(name="banks", bufs=2))
+        sums_1 = stack.enter_context(tc.psum_pool(name="sums_1", bufs=EARLY))
+        sums_0 = stack.enter_context(tc.psum_pool(name="sums_0", bufs=N_TILES - FLIPPED))
+        flipped = stack.enter_context(tc.psum_pool(name="flipped", bufs=2))
         stack.enter_context(tc.manual_schedule())
 
-        def scenes(t):
-            return slice(t * TILE_SCENES, (t + 1) * TILE_SCENES)
+        def tile_rows(tensor, t):
+            return tensor.rearrange("b (k t) c -> t (b k) c", t=TOKEN_TILES)[t]
 
         identity = keep.tile([P, P], F32)
         make_identity(nc, identity[:])
@@ -72,80 +68,130 @@ def tile_differentiablelogicmachine_pb_kernel(tc, x0, x1, x2, W1_words, W1_scale
         nc.vector.memset(nullary[:].bitcast(I32), 0)
         table_loaded = keep.tile([P, 1], F32)
         nc.scalar.activation(out=table_loaded[:], in_=nullary[:, 0:1], func=ACT.Sigmoid)
+        bias_rows = keep.tile([P, P], F32)
+        nc.gpsimd.memset(bias_rows[:], 0.0)
+        without_flat = keep.tile([P, TILE_OBJECTS * (P + 1)], F32)
+        without = without_flat[:, 0 : TILE_OBJECTS * P].rearrange("p (s k) -> p s k", k=P)
+        nc.vector.tensor_copy(out=without, in_=identity[:].unsqueeze(1).to_broadcast([P, TILE_OBJECTS, P]))
+        nc.vector.memset(diagonal(without_flat, P, 1), 0.0)
         w_scales = keep.tile([P, GROUPS, OUT], U8, align_bytes=64)
         nc.vector.memset(w_scales[:].rearrange("p g n -> p (g n)").bitcast(I32), 0)
-        without_flat = keep.tile([P, OBJECTS * (P + 1)], F32)
-        without = without_flat[:, 0 : OBJECTS * P].rearrange("p (j k) -> p j k", k=P)
-        for q in range(QUARTERS):
-            four = without[:, q * QUARTER : (q + 1) * QUARTER, :]
-            nc.vector.tensor_copy(out=four, in_=identity[:].unsqueeze(1).to_broadcast([P, QUARTER, P]))
-            first = q * QUARTER
-            nc.vector.memset(diagonal(without_flat, P, 1)[:, first : first + QUARTER, :, :], 0.0)
 
-        relations = {}
+        relations = [keep.tile([P, OBJECTS, CH], BF16, name="relations_%d" % t) for t in range(TOKEN_TILES)]
 
-        def load_relations(t):
-            for j in range(0, OBJECTS, BANK_ROWS):
-                token_major = keep.tile([P, BANK_ROWS, CH], BF16, name="relations_%d_%d" % (t, j))
-                nc.sync.dma_start(
-                    out=token_major[:].rearrange("p j c -> p (j c)"),
-                    in_=x2[scenes(t), :, j : j + BANK_ROWS, :].rearrange("b i j c -> (b i) (j c)"),
-                )
-                relations[(t, j)] = token_major
+        def load_relations(t, first, count):
+            rows = tile_rows(x2.rearrange("b i j c -> b i (j c)"), t)
+            nc.sync.dma_start(
+                out=relations[t][:, first : first + count, :].rearrange("p j c -> p (j c)"),
+                in_=rows[:, first * CH : (first + count) * CH],
+            )
 
-        load_relations(0)
+        head = [keep.tile([P, 2, CH], BF16, name="head_%d" % k) for k in range(CHUNK)]
+
+        def load_head(c, is_far):
+            rows = x2.rearrange("b (k t) (j f) c -> t f (b k) j c", t=TOKEN_TILES, f=2)[0, is_far]
+            nc.sync.dma_start(out=head[2 * c + is_far][:], in_=rows[:, 2 * c : 2 * c + 2, :])
+
+        w_words = [keep.tile([P, GROUPS, 2 * N_TILE], U8, name="w_words_%d" % n, align_bytes=64) for n in range(N_TILES)]
+
+        def load_weights(n):
+            cols = slice(2 * n * N_TILE, 2 * (n + 1) * N_TILE)
+            nc.sync.dma_start(
+                out=w_words[n][:].bitcast(I32), in_=W1_words[:, :, cols].rearrange("g p n -> p g n").bitcast(I32)
+            )
+
+        for c in range(2):
+            load_head(c, 1)
+        for c in range(2):
+            load_head(c, 0)
+        for c in range(2, CHUNKS):
+            load_relations(0, c * CHUNK, CHUNK)
+        bias_short = keep.tile([OUT // P, P], BF16)
+        nc.sync.dma_start(out=bias_short[:], in_=b1.rearrange("(m k) -> m k", k=P))
         nc.sync.dma_start(out=nullary[0:SCENES, :], in_=x0)
         unary = keep.tile([P, TOKEN_TILES, CH], BF16)
         for t in range(TOKEN_TILES):
-            nc.sync.dma_start(out=unary[:, t, :], in_=x1[scenes(t), :, :].rearrange("b i c -> (b i) c"))
-        load_relations(1)
+            nc.sync.dma_start(out=unary[:, t, :], in_=tile_rows(x1, t))
         for r in range(4):
             nc.sync.dma_start(
                 out=w_scales[r:P:32, :, :].bitcast(I32),
                 in_=W1_scales[:, r:16:4, :].rearrange("g q n -> q g n").bitcast(I32),
             )
-        w_words = keep.tile([P, GROUPS, 2 * OUT], U8, align_bytes=64)
-        for g in range(GROUPS):
-            nc.sync.dma_start(out=w_words[:, g, :].bitcast(I32), in_=W1_words[g].bitcast(I32))
+        for c in range(CHUNKS):
+            load_relations(1, c * CHUNK, CHUNK)
+        for n in range(N_TILES):
+            load_weights(n)
         bias = keep.tile([P, OUT], BF16)
         nc.sync.dma_start(out=bias[:], in_=b1.partition_broadcast(P))
 
-        turned = {}
-        turned_flat = [keep.tile([P, OBJECTS * (CH + PACK)], BF16, name="turned_%d" % t) for t in range(TOKEN_TILES)]
+        def turn(src, bank_part, selector):
+            for u in range(WORD_HALVES):
+                nc.tensor.transpose(bank_part[:, u, :], src.bitcast(F32)[:, u : CH // 2 : WORD_HALVES], selector)
 
-        def turn_relations(t):
-            for q in range(QUARTERS):
-                first = q * QUARTER
-                rows = turned_flat[t][:, first * CH : (first + QUARTER) * CH].rearrange("p (s k) -> p s k", k=CH)
-                for s in range(0, QUARTER, BANK_ROWS):
-                    j = q * QUARTER + s
-                    to_channel_major(
-                        nc,
-                        banks,
-                        [without[:, j + k, :] for k in range(BANK_ROWS)],
-                        relations[(t, j)][:],
-                        rows[:, s : s + BANK_ROWS, :],
-                    )
-                turned[(t, q)] = rows
-
-        f1 = keep.tile([P, GROUPS * TOKEN_TILES, CH], BF16, align_bytes=64)
-        f1_words = keep.tile([P, GROUPS * TOKEN_TILES, P], U32, align_bytes=64)
-        f1_scales = keep.tile([P, GROUPS * TOKEN_TILES, P], U8, align_bytes=64)
-
-        turn_relations(0)
-        scene_words = banks.tile([P, WORD_HALVES, P], F32, tag="bank")
-        for u in range(WORD_HALVES):
-            nc.tensor.transpose(scene_words[:, u, :], nullary[:].bitcast(F32)[:, u : CH // 2 : WORD_HALVES], identity[:])
-        for t in range(TOKEN_TILES):
+        def turn_two(two, selectors, dst):
+            bank = banks.tile([P, BANK_ROWS, WORD_HALVES, P], F32, tag="bank")
+            for s in range(BANK_ROWS):
+                turn(two[s], bank[:, s, :, :], selectors[s])
             nc.scalar.copy(
-                out=f1[:, t, :].bitcast(F32).rearrange("p (b i u) -> p b i u", i=OBJECTS, u=WORD_HALVES),
-                in_=scene_words[:, :, scenes(t)]
+                out=dst.bitcast(F32).rearrange("p s (k u) -> p s k u", u=WORD_HALVES),
+                in_=bank[:].rearrange("p s u k -> p s k u"),
+            )
+
+        near_flat = [
+            keep.tile([P, TILE_OBJECTS * (CH + PACK)], BF16, name="near_%d" % t) for t in range(TOKEN_TILES)
+        ]
+        far_turned = keep.tile([P, TOKEN_TILES, len(KINDS), CH], BF16)
+
+        def near(t, first, count):
+            return near_flat[t][:, first * CH : (first + count) * CH].rearrange("p (s k) -> p s k", k=CH)
+
+        def far(t, first, count):
+            if t == 0 and first < CHUNK:
+                return head[first + 1][:]
+            j = 2 * first + 1 - t
+            return relations[t][:, j : j + 2 * count - 1 : 2, :]
+
+        def turn_near(t, c):
+            s = c * BANK_ROWS
+            turn_two(
+                [head[s][:, k, :] if t == 0 and c < 2 else relations[t][:, 2 * (s + k) + t, :] for k in range(BANK_ROWS)],
+                [without[:, s + k, :] for k in range(BANK_ROWS)],
+                near(t, s, BANK_ROWS),
+            )
+
+        def turn_far(t, reduced):
+            turn_two([reduced[k] for k in KINDS], [identity[:]] * BANK_ROWS, far_turned[:, t, :, :])
+
+        f1 = keep.tile([P, SLOTS, CH], BF16, align_bytes=64)
+        f1_words = keep.tile([P, SLOTS, P], U32, align_bytes=64)
+        f1_scales = keep.tile([P, SLOTS, P], U8, align_bytes=64)
+
+        def turn_inputs():
+            scene_words = banks.tile([P, WORD_HALVES, P], F32, tag="bank")
+            turn(nullary[:], scene_words, identity[:])
+            nc.scalar.copy(
+                out=f1[:, f1_slot(0, 0), :].bitcast(F32).rearrange(
+                    "p (b i u) -> p b i u", i=TILE_OBJECTS, u=WORD_HALVES
+                ),
+                in_=scene_words[:, :, 0:SCENES]
                 .rearrange("p u b -> p b u")
                 .unsqueeze(2)
-                .to_broadcast([P, TILE_SCENES, OBJECTS, WORD_HALVES]),
+                .to_broadcast([P, SCENES, TILE_OBJECTS, WORD_HALVES]),
             )
-        to_channel_major(nc, banks, [identity[:]] * BANK_ROWS, unary[:], f1[:, TOKEN_TILES : 2 * TOKEN_TILES, :])
-        turn_relations(1)
+            first = f1_slot(1, 0)
+            turn_two(
+                [unary[:, t, :] for t in range(TOKEN_TILES)],
+                [identity[:]] * BANK_ROWS,
+                f1[:, first : first + TOKEN_TILES, :],
+            )
+
+        bias_columns = keep.tile([P, OUT // P], F32)
+
+        def turn_bias():
+            nc.scalar.copy(out=bias_rows[0 : OUT // P, :], in_=bias_short[:])
+            bias_words = banks.tile([P, P], F32, tag="bank")
+            nc.tensor.transpose(bias_words[:], bias_rows[:], identity[:])
+            nc.scalar.copy(out=bias_columns[:], in_=bias_words[:, 0 : OUT // P])
 
         def quantise(first, count):
             slots = slice(first, first + count)
@@ -155,79 +201,195 @@ def tile_differentiablelogicmachine_pb_kernel(tc, x0, x1, x2, W1_words, W1_scale
                 in_=f1[:, slots, :].rearrange("p q k -> p (q k)"),
             )
 
-        def halve(t, q, kind):
-            pair = work.tile([P, 2, CH], BF16, tag="pair_%d" % kind)
-            rows = turned[(t, q)]
-            nc.vector.tensor_tensor(out=pair[:], in0=rows[:, 0:2, :], in1=rows[:, 2:4, :], op=OPS[kind])
-            return pair
+        def best_of(kind, dst, a, b):
+            nc.vector.tensor_tensor(out=dst, in0=a, in1=b, op=OPS[kind])
 
-        def join(kind, best, pair):
-            joined = work.tile([P, 2, CH], BF16, tag="best_%d" % kind)
-            nc.vector.tensor_tensor(out=joined[:], in0=best[:], in1=pair[:], op=OPS[kind])
-            return joined
+        def refill(t, first, count):
+            nc.gpsimd.memset(diagonal(near_flat[t], CH, PACK)[:, first : first + count, :, :], 1.0)
 
-        def refill(t, q):
-            first = q * QUARTER
-            nc.vector.memset(diagonal(turned_flat[t], CH, PACK)[:, first : first + QUARTER, :, :], 1.0)
-
-        def last_step(t, kind, best):
-            nc.vector.tensor_tensor(
-                out=f1[:, (2 + kind) * TOKEN_TILES + t, :], in0=best[:, 0, :], in1=best[:, 1, :], op=OPS[kind]
-            )
-
-        def reduce_tile(t, meanwhile):
-            for q in range(QUARTERS):
-                high = halve(t, q, MAX)
-                if q == 1:
-                    low_best = low
-                if q > 1:
-                    low_best = join(MIN, low_best, low)
-                refill(t, q)
-                high_best = high if q == 0 else join(MAX, high_best, high)
-                low = halve(t, q, MIN)
-            last_step(t, MAX, high_best)
-            low_best = join(MIN, low_best, low)
-            quantise(2 * TOKEN_TILES + t, 1)
-            meanwhile()
-            last_step(t, MIN, low_best)
-            quantise(3 * TOKEN_TILES + t, 1)
+        def scratch(t, label, rows):
+            return [keep.tile([P, rows, CH], BF16, name="%s_%d_%d" % (label, t, k)) for k in KINDS]
 
         sums = {}
 
         def one_pass(t, g, n):
             if g == 0:
-                pool = sums_0 if t == 0 else banks
+                pool = sums_0 if t == 0 else sums_1 if n < EARLY else banks
                 bank = pool.tile([P, N_TILE], F32, tag="bank")
                 sums[(t, n)] = bank
-            slot = g * TOKEN_TILES + t
+            slot = f1_slot(g, t)
             nc.tensor.matmul_mx(
                 out=sums[(t, n)][:],
                 lhsT=f1_words[:, slot, :].bitcast(FP8X4),
                 lhsT_scale=f1_scales[:, slot, :],
-                rhs=w_words[:, g, 2 * n * N_TILE : 2 * (n + 1) * N_TILE].bitcast(FP4X4),
+                rhs=w_words[n][:, g, :].bitcast(FP4X4),
                 rhs_scale=w_scales[:, g, n * N_TILE : (n + 1) * N_TILE],
                 start=(g == 0),
                 stop=(g == GROUPS - 1),
             )
 
-        def finish(t, some_banks):
-            for n in some_banks:
-                cols = slice(n * N_TILE, (n + 1) * N_TILE)
-                result = results.tile([P, N_TILE], F32)
-                nc.vector.tensor_tensor(out=result[:], in0=sums[(t, n)][:], in1=bias[:, cols], op=ALU.add)
-                nc.scalar.activation(out=result[:], in_=result[:], func=ACT.Sigmoid)
-                nc.sync.dma_start(out=out[scenes(t), :, cols].rearrange("b i o -> (b i) o"), in_=result[:])
+        def flipped_passes(n):
+            bank = flipped.tile([P, N_TILE // P, P], F32, tag="bank")
+            for m in range(N_TILE // P):
+                first = n * N_TILE + m * P
+                for g in range(GROUPS):
+                    slot = f1_slot(g, 0)
+                    nc.tensor.matmul_mx(
+                        out=bank[:, m, :],
+                        lhsT=w_words[n][:, g, 2 * m * P : 2 * (m + 1) * P].bitcast(FP4X4),
+                        lhsT_scale=w_scales[:, g, first : first + P],
+                        rhs=f1_words[:, slot, :].bitcast(FP8X4),
+                        rhs_scale=f1_scales[:, slot, :],
+                        start=(g == 0),
+                        stop=(g == GROUPS - 1),
+                    )
+            sums[(0, n)] = bank
 
-        reduce_tile(0, lambda: quantise(0, 2 * TOKEN_TILES))
-        for n in range(N_TILES):
-            for g in range(GROUPS):
-                one_pass(0, g, n)
-        for g in range(2):
-            for n in range(N_TILES):
-                one_pass(1, g, n)
-        reduce_tile(1, lambda: finish(0, range(N_TILES // 2)))
+        activated = {}
+
+        def flipped_sigmoids(n):
+            result = keep.tile([P, N_TILE // P, P], F32, name="activated_%d" % n)
+            for m in range(N_TILE // P):
+                column = n * (N_TILE // P) + m
+                nc.scalar.activation(
+                    out=result[:, m, :],
+                    in_=sums[(0, n)][:, m, :],
+                    func=ACT.Sigmoid,
+                    bias=bias_columns[:, column : column + 1],
+                )
+            activated[n] = result
+
+        def flip_back(n):
+            bank = flipped.tile([P, N_TILE // P, P], F32, tag="bank")
+            for m in range(N_TILE // P):
+                nc.tensor.transpose(bank[:, m, :], activated[n][:, m, :], identity[:])
+            result = keep.tile([P, N_TILE], F32, name="result_0_%d" % n)
+            nc.scalar.copy(out=result[:], in_=bank[:].rearrange("p m k -> p (m k)"))
+            cols = slice(n * N_TILE, (n + 1) * N_TILE)
+            nc.sync.dma_start(out=tile_rows(out, 0)[:, cols], in_=result[:])
+
+        def finish(t, n, parts=1):
+            width = N_TILE // parts
+            result = keep.tile([P, N_TILE], F32, name="result_%d_%d" % (t, n))
+            for first in range(0, N_TILE, width):
+                part = result[:, first : first + width]
+                cols = slice(n * N_TILE + first, n * N_TILE + first + width)
+                nc.vector.tensor_tensor(
+                    out=part, in0=sums[(t, n)][:, first : first + width], in1=bias[:, cols], op=ALU.add
+                )
+                nc.scalar.activation(out=part, in_=part, func=ACT.Sigmoid)
+                nc.sync.dma_start(out=tile_rows(out, t)[:, cols], in_=part)
+
+
+        def fold(k, dst, src):
+            half = src.shape[1] // 2
+            best_of(k, dst, src[:, 0:half, :], src[:, half : 2 * half, :])
+
+        def whole(t, k, near_best, far_best_turned):
+            best_of(k, f1[:, f1_slot(2 + k, t), :], near_best[k][:, 0, :], far_best_turned)
+
+        far_pairs = scratch(0, "far_pairs", CHUNKS)
+        near_pairs = scratch(0, "near_pairs", CHUNKS)
+        far_fours = scratch(0, "far_fours", 2)
+        near_fours = scratch(0, "near_fours", 2)
+        far_best = scratch(0, "far_best", 1)
+        near_best = scratch(0, "near_best", 1)
+
+        def far_pair(c):
+            for k in KINDS:
+                fold(k, far_pairs[k][:, c : c + 1, :], far(0, 2 * c, 2))
+
+        def near_pair(k, c, count=1):
+            fold(k, near_pairs[k][:, c : c + count, :], near(0, 2 * c, 2 * count))
+            if k == MAX:
+                refill(0, 2 * c, 2 * count)
+
+        def far_four(h):
+            for k in KINDS:
+                fold(k, far_fours[k][:, h : h + 1, :], far_pairs[k][:, 2 * h : 2 * h + 2, :])
+
+        for c in range(CHUNKS):
+            turn_near(0, c)
+        turn_inputs()
+        turn_bias()
+        far_pair(0)
+        far_pair(1)
+        far_four(0)
+        near_pair(MAX, 0)
+        far_pair(2)
+        near_pair(MAX, 1)
+        near_pair(MIN, 0)
+        far_pair(3)
+        near_pair(MIN, 1)
+        far_four(1)
+        near_pair(MAX, 2, 2)
+        for k in KINDS:
+            fold(k, far_best[k][:], far_fours[k][:])
+        quantise(f1_slot(0, 0), 1)
+        quantise(f1_slot(1, 0), TOKEN_TILES)
+
+        def early_passes(t, n):
+            for g in range(2):
+                one_pass(t, g, n)
+
+        turn_far(0, [far_best[k][:, 0, :] for k in KINDS])
+        near_pair(MIN, 2, 2)
+        for c in range(CHUNKS):
+            turn_near(1, c)
+        for n in range(EARLY):
+            early_passes(1, n)
+        for k in KINDS:
+            fold(k, near_fours[k][:], near_pairs[k][:])
+        for k in KINDS:
+            fold(k, near_best[k][:], near_fours[k][:])
+        for k in KINDS:
+            whole(0, k, near_best, far_turned[:, 0, k, :])
+
+        far_fours = scratch(1, "far_fours", 4)
+        near_fours = scratch(1, "near_fours", 4)
+        far_pairs = scratch(1, "far_pairs", 2)
+        near_pairs = scratch(1, "near_pairs", 2)
+        far_best = scratch(1, "far_best", 1)
+        near_best = scratch(1, "near_best", 1)
+
+        fold(MAX, far_fours[MAX][:], far(1, 0, TILE_OBJECTS))
+        quantise(f1_slot(2, 0), len(KINDS))
+        fold(MIN, far_fours[MIN][:], far(1, 0, TILE_OBJECTS))
+        for n in range(FLIPPED):
+            flipped_passes(n)
+            flipped_sigmoids(n)
+        fold(MAX, near_fours[MAX][:], near(1, 0, TILE_OBJECTS))
+        refill(1, 0, TILE_OBJECTS)
+        for k in KINDS:
+            fold(k, far_pairs[k][:], far_fours[k][:])
+        for k in KINDS:
+            fold(k, far_best[k][:], far_pairs[k][:])
+        for n in range(FLIPPED):
+            flip_back(n)
+        turn_far(1, [far_best[k][:, 0, :] for k in KINDS])
+
+        def late_passes(t, n):
+            for g in range(2, GROUPS):
+                one_pass(t, g, n)
+
+        for n in range(FLIPPED, N_TILES):
+            early_passes(0, n)
+            late_passes(0, n)
+        for n in range(EARLY, N_TILES):
+            early_passes(1, n)
+        fold(MIN, near_fours[MIN][:], near(1, 0, TILE_OBJECTS))
+        fold(MAX, near_pairs[MAX][:], near_fours[MAX][:])
+        fold(MIN, near_pairs[MIN][:], near_fours[MIN][:])
+        fold(MAX, near_best[MAX][:], near_pairs[MAX][:])
+        fold(MIN, near_best[MIN][:], near_pairs[MIN][:])
+        for k in KINDS:
+            whole(1, k, near_best, far_turned[:, 1, k, :])
+        quantise(f1_slot(2, 1), 1)
+        quantise(f1_slot(3, 1), 1)
         for g in range(2, GROUPS):
             for n in range(N_TILES):
                 one_pass(1, g, n)
-        finish(0, range(N_TILES // 2, N_TILES))
-        finish(1, range(N_TILES))
+        finish(0, 2)
+        finish(0, 3)
+        for n in range(N_TILES):
+            finish(1, n, 2 if n == N_TILES - 1 else 1)

@@ -68,6 +68,10 @@ def tile_differentiablelogicmachine_pb_kernel(tc, x0, x1, x2, W1_words, W1_scale
         nc.vector.memset(nullary[:].bitcast(I32), 0)
         table_loaded = keep.tile([P, 1], F32)
         nc.scalar.activation(out=table_loaded[:], in_=nullary[:, 0:1], func=ACT.Sigmoid)
+        ones = keep.tile([P, P], BF16)
+        nc.gpsimd.memset(ones[:], 1.0)
+        bias_row = keep.tile([P, OUT], BF16)
+        nc.gpsimd.memset(bias_row[:].bitcast(I32), 0)
         bias_rows = keep.tile([P, P], F32)
         nc.gpsimd.memset(bias_rows[:], 0.0)
         without_flat = keep.tile([P, TILE_OBJECTS * (P + 1)], F32)
@@ -104,6 +108,7 @@ def tile_differentiablelogicmachine_pb_kernel(tc, x0, x1, x2, W1_words, W1_scale
             load_head(c, 1)
         for c in range(2):
             load_head(c, 0)
+        nc.sync.dma_start(out=bias_row[0:1, :], in_=b1.unsqueeze(0))
         for c in range(2, CHUNKS):
             load_relations(0, c * CHUNK, CHUNK)
         bias_short = keep.tile([OUT // P, P], BF16)
@@ -112,17 +117,18 @@ def tile_differentiablelogicmachine_pb_kernel(tc, x0, x1, x2, W1_words, W1_scale
         unary = keep.tile([P, TOKEN_TILES, CH], BF16)
         for t in range(TOKEN_TILES):
             nc.sync.dma_start(out=unary[:, t, :], in_=tile_rows(x1, t))
+        for c in range(2):
+            load_relations(1, c * CHUNK, CHUNK)
         for r in range(4):
             nc.sync.dma_start(
                 out=w_scales[r:P:32, :, :].bitcast(I32),
                 in_=W1_scales[:, r:16:4, :].rearrange("g q n -> q g n").bitcast(I32),
             )
-        for c in range(CHUNKS):
+        load_weights(0)
+        for c in range(2, CHUNKS):
             load_relations(1, c * CHUNK, CHUNK)
-        for n in range(N_TILES):
+        for n in range(1, N_TILES):
             load_weights(n)
-        bias = keep.tile([P, OUT], BF16)
-        nc.sync.dma_start(out=bias[:], in_=b1.partition_broadcast(P))
 
         def turn(src, bank_part, selector):
             for u in range(WORD_HALVES):
@@ -192,6 +198,14 @@ def tile_differentiablelogicmachine_pb_kernel(tc, x0, x1, x2, W1_words, W1_scale
             bias_words = banks.tile([P, P], F32, tag="bank")
             nc.tensor.transpose(bias_words[:], bias_rows[:], identity[:])
             nc.scalar.copy(out=bias_columns[:], in_=bias_words[:, 0 : OUT // P])
+
+        bias = keep.tile([P, OUT], BF16)
+
+        def spread_bias(n):
+            cols = slice(n * N_TILE, (n + 1) * N_TILE)
+            bank = sums_0.tile([P, N_TILE], F32, tag="bank")
+            nc.tensor.matmul(bank[:], lhsT=ones[:], rhs=bias_row[:, cols], start=True, stop=True)
+            nc.scalar.copy(out=bias[:, cols], in_=bank[:])
 
         def quantise(first, count):
             slots = slice(first, first + count)
@@ -310,8 +324,11 @@ def tile_differentiablelogicmachine_pb_kernel(tc, x0, x1, x2, W1_words, W1_scale
 
         for c in range(CHUNKS):
             turn_near(0, c)
+            if c > 0:
+                spread_bias(c - 1)
         turn_inputs()
         turn_bias()
+        spread_bias(N_TILES - 1)
         far_pair(0)
         far_pair(1)
         far_four(0)
@@ -328,16 +345,10 @@ def tile_differentiablelogicmachine_pb_kernel(tc, x0, x1, x2, W1_words, W1_scale
         quantise(f1_slot(0, 0), 1)
         quantise(f1_slot(1, 0), TOKEN_TILES)
 
-        def early_passes(t, n):
-            for g in range(2):
-                one_pass(t, g, n)
-
         turn_far(0, [far_best[k][:, 0, :] for k in KINDS])
         near_pair(MIN, 2, 2)
-        for c in range(CHUNKS):
+        for c in range(2):
             turn_near(1, c)
-        for n in range(EARLY):
-            early_passes(1, n)
         for k in KINDS:
             fold(k, near_fours[k][:], near_pairs[k][:])
         for k in KINDS:
@@ -352,44 +363,64 @@ def tile_differentiablelogicmachine_pb_kernel(tc, x0, x1, x2, W1_words, W1_scale
         far_best = scratch(1, "far_best", 1)
         near_best = scratch(1, "near_best", 1)
 
-        fold(MAX, far_fours[MAX][:], far(1, 0, TILE_OBJECTS))
-        quantise(f1_slot(2, 0), len(KINDS))
-        fold(MIN, far_fours[MIN][:], far(1, 0, TILE_OBJECTS))
-        for n in range(FLIPPED):
-            flipped_passes(n)
-            flipped_sigmoids(n)
-        fold(MAX, near_fours[MAX][:], near(1, 0, TILE_OBJECTS))
-        refill(1, 0, TILE_OBJECTS)
-        for k in KINDS:
-            fold(k, far_pairs[k][:], far_fours[k][:])
-        for k in KINDS:
-            fold(k, far_best[k][:], far_pairs[k][:])
-        for n in range(FLIPPED):
-            flip_back(n)
-        turn_far(1, [far_best[k][:, 0, :] for k in KINDS])
+        def far_half(k, h):
+            fold(k, far_fours[k][:, 2 * h : 2 * h + 2, :], far(1, 4 * h, 4))
+
+        def near_half(k, h):
+            fold(k, near_fours[k][:, 2 * h : 2 * h + 2, :], near(1, 4 * h, 4))
+            if k == MAX:
+                refill(1, 4 * h, 4)
+
+        def early_passes(t, n):
+            for g in range(2):
+                one_pass(t, g, n)
 
         def late_passes(t, n):
             for g in range(2, GROUPS):
                 one_pass(t, g, n)
 
-        for n in range(FLIPPED, N_TILES):
-            early_passes(0, n)
-            late_passes(0, n)
-        for n in range(EARLY, N_TILES):
-            early_passes(1, n)
-        fold(MIN, near_fours[MIN][:], near(1, 0, TILE_OBJECTS))
-        fold(MAX, near_pairs[MAX][:], near_fours[MAX][:])
-        fold(MIN, near_pairs[MIN][:], near_fours[MIN][:])
-        fold(MAX, near_best[MAX][:], near_pairs[MAX][:])
-        fold(MIN, near_best[MIN][:], near_pairs[MIN][:])
+        far_half(MAX, 0)
+        quantise(f1_slot(2, 0), len(KINDS))
+        far_half(MIN, 0)
+        early_passes(1, 0)
+        flipped_passes(0)
+        turn_near(1, 2)
+        flipped_sigmoids(0)
+        turn_near(1, 3)
+        near_half(MAX, 0)
+        early_passes(1, 1)
+        flipped_passes(1)
+        flipped_sigmoids(1)
+        flip_back(0)
         for k in KINDS:
-            whole(1, k, near_best, far_turned[:, 1, k, :])
+            far_half(k, 1)
+        near_half(MIN, 0)
+        for k in KINDS:
+            fold(k, far_pairs[k][:], far_fours[k][:])
+        near_half(MAX, 1)
+        for k in KINDS:
+            fold(k, far_best[k][:], far_pairs[k][:])
+        early_passes(0, 2)
+        late_passes(0, 2)
+        flip_back(1)
+        turn_far(1, [far_best[k][:, 0, :] for k in KINDS])
+        early_passes(0, 3)
+        late_passes(0, 3)
+        for n in range(2, N_TILES):
+            early_passes(1, n)
+        fold(MAX, near_pairs[MAX][:], near_fours[MAX][:])
+        near_half(MIN, 1)
+        fold(MAX, near_best[MAX][:], near_pairs[MAX][:])
+        fold(MIN, near_pairs[MIN][:], near_fours[MIN][:])
+        whole(1, MAX, near_best, far_turned[:, 1, MAX, :])
+        fold(MIN, near_best[MIN][:], near_pairs[MIN][:])
         quantise(f1_slot(2, 1), 1)
+        whole(1, MIN, near_best, far_turned[:, 1, MIN, :])
+        finish(0, 2)
         quantise(f1_slot(3, 1), 1)
         for g in range(2, GROUPS):
             for n in range(N_TILES):
                 one_pass(1, g, n)
-        finish(0, 2)
         finish(0, 3)
         for n in range(N_TILES):
             finish(1, n, 2 if n == N_TILES - 1 else 1)

@@ -28,7 +28,7 @@ CHUNKS = OBJECTS // CHUNK
 BANK_ROWS = 2
 N_TILE = 512
 N_TILES = OUT // N_TILE
-FLIPPED = 2
+FLIPPED = 1
 EARLY = 2
 SLOTS = 7
 
@@ -56,7 +56,7 @@ def tile_differentiablelogicmachine_pb_kernel(tc, x0, x1, x2, W1_words, W1_scale
         banks = stack.enter_context(tc.psum_pool(name="banks", bufs=2))
         sums_1 = stack.enter_context(tc.psum_pool(name="sums_1", bufs=EARLY))
         sums_0 = stack.enter_context(tc.psum_pool(name="sums_0", bufs=N_TILES - FLIPPED))
-        flipped = stack.enter_context(tc.psum_pool(name="flipped", bufs=2))
+        flipped = stack.enter_context(tc.psum_pool(name="flipped", bufs=1))
         stack.enter_context(tc.manual_schedule())
 
         def tile_rows(tensor, t):
@@ -106,7 +106,6 @@ def tile_differentiablelogicmachine_pb_kernel(tc, x0, x1, x2, W1_words, W1_scale
 
         for c in range(2):
             load_head(c, 1)
-        for c in range(2):
             load_head(c, 0)
         nc.sync.dma_start(out=bias_row[0:1, :], in_=b1.unsqueeze(0))
         for c in range(2, CHUNKS):
@@ -117,15 +116,13 @@ def tile_differentiablelogicmachine_pb_kernel(tc, x0, x1, x2, W1_words, W1_scale
         unary = keep.tile([P, TOKEN_TILES, CH], BF16)
         for t in range(TOKEN_TILES):
             nc.sync.dma_start(out=unary[:, t, :], in_=tile_rows(x1, t))
-        for c in range(2):
-            load_relations(1, c * CHUNK, CHUNK)
         for r in range(4):
             nc.sync.dma_start(
                 out=w_scales[r:P:32, :, :].bitcast(I32),
                 in_=W1_scales[:, r:16:4, :].rearrange("g q n -> q g n").bitcast(I32),
             )
         load_weights(0)
-        for c in range(2, CHUNKS):
+        for c in range(CHUNKS):
             load_relations(1, c * CHUNK, CHUNK)
         for n in range(1, N_TILES):
             load_weights(n)
@@ -324,11 +321,7 @@ def tile_differentiablelogicmachine_pb_kernel(tc, x0, x1, x2, W1_words, W1_scale
 
         for c in range(CHUNKS):
             turn_near(0, c)
-            if c > 0:
-                spread_bias(c - 1)
         turn_inputs()
-        turn_bias()
-        spread_bias(N_TILES - 1)
         far_pair(0)
         far_pair(1)
         far_four(0)
@@ -343,12 +336,23 @@ def tile_differentiablelogicmachine_pb_kernel(tc, x0, x1, x2, W1_words, W1_scale
         for k in KINDS:
             fold(k, far_best[k][:], far_fours[k][:])
         quantise(f1_slot(0, 0), 1)
+        near_pair(MIN, 2, 2)
         quantise(f1_slot(1, 0), TOKEN_TILES)
 
+        def early_passes(t, n):
+            for g in range(2):
+                one_pass(t, g, n)
+
+        def late_passes(t, n):
+            for g in range(2, GROUPS):
+                one_pass(t, g, n)
+
         turn_far(0, [far_best[k][:, 0, :] for k in KINDS])
-        near_pair(MIN, 2, 2)
+        early_passes(1, 0)
+        turn_bias()
         for c in range(2):
             turn_near(1, c)
+            spread_bias(c)
         for k in KINDS:
             fold(k, near_fours[k][:], near_pairs[k][:])
         for k in KINDS:
@@ -371,26 +375,19 @@ def tile_differentiablelogicmachine_pb_kernel(tc, x0, x1, x2, W1_words, W1_scale
             if k == MAX:
                 refill(1, 4 * h, 4)
 
-        def early_passes(t, n):
-            for g in range(2):
-                one_pass(t, g, n)
-
-        def late_passes(t, n):
-            for g in range(2, GROUPS):
-                one_pass(t, g, n)
-
         far_half(MAX, 0)
         quantise(f1_slot(2, 0), len(KINDS))
         far_half(MIN, 0)
-        early_passes(1, 0)
+        spread_bias(2)
         flipped_passes(0)
+        spread_bias(3)
         turn_near(1, 2)
         flipped_sigmoids(0)
         turn_near(1, 3)
         near_half(MAX, 0)
         early_passes(1, 1)
-        flipped_passes(1)
-        flipped_sigmoids(1)
+        early_passes(0, 1)
+        late_passes(0, 1)
         flip_back(0)
         for k in KINDS:
             far_half(k, 1)
@@ -401,15 +398,15 @@ def tile_differentiablelogicmachine_pb_kernel(tc, x0, x1, x2, W1_words, W1_scale
         for k in KINDS:
             fold(k, far_best[k][:], far_pairs[k][:])
         early_passes(0, 2)
-        late_passes(0, 2)
-        flip_back(1)
         turn_far(1, [far_best[k][:, 0, :] for k in KINDS])
+        late_passes(0, 2)
         early_passes(0, 3)
         late_passes(0, 3)
         for n in range(2, N_TILES):
             early_passes(1, n)
         fold(MAX, near_pairs[MAX][:], near_fours[MAX][:])
         near_half(MIN, 1)
+        finish(0, 1)
         fold(MAX, near_best[MAX][:], near_pairs[MAX][:])
         fold(MIN, near_pairs[MIN][:], near_fours[MIN][:])
         whole(1, MAX, near_best, far_turned[:, 1, MAX, :])

from contextlib import ExitStack

import concourse.mybir as mybir
from concourse.masks import make_identity

BF16 = mybir.dt.bfloat16
F32 = mybir.dt.float32
I32 = mybir.dt.int32
U8 = mybir.dt.uint8
U32 = mybir.dt.uint32
FP8X4 = mybir.dt.float8_e4m3fn_x4
FP4X4 = mybir.dt.float4_e2m1fn_x4
ALU = mybir.AluOpType
ACT = mybir.ActivationFunctionType

P = 128
SCENES = 16
OBJECTS = 16
CH = 512
OUT = 2048
PACK = 4
WORD_HALVES = 2
GROUPS = 4
TOKEN_TILES = 2
TILE_OBJECTS = P // SCENES
CHUNK = 4
CHUNKS = OBJECTS // CHUNK
BANK_ROWS = 2
N_TILE = 512
N_TILES = OUT // N_TILE
FLIPPED = 1
EARLY = 2
SLOTS = 7

FLOPS = 2 * SCENES * OBJECTS * GROUPS * CH * OUT

MAX = 0
MIN = 1
KINDS = (MAX, MIN)
OPS = (ALU.max, ALU.min)


def f1_slot(g, t):
    return (0, 1 + t, 3 + 2 * t, 4 + 2 * t)[g]


def diagonal(flat, row, run):
    rows = flat[:, 0 : TILE_OBJECTS * (row + run)].rearrange("p (s k) -> p s k", k=row + run)
    return rows[:, :, 0:row].rearrange("p s (b k) -> p s b k", b=SCENES)[:, :, :, 0:run]


def tile_differentiablelogicmachine_pb_kernel(tc, x0, x1, x2, W1_words, W1_scales, b1, out):
    nc = tc.nc
    with ExitStack() as stack:
        keep = stack.enter_context(tc.tile_pool(name="keep", bufs=1))
        banks = stack.enter_context(tc.psum_pool(name="banks", bufs=2))
        sums_1 = stack.enter_context(tc.psum_pool(name="sums_1", bufs=EARLY))
        sums_0 = stack.enter_context(tc.psum_pool(name="sums_0", bufs=N_TILES - FLIPPED))
        flipped = stack.enter_context(tc.psum_pool(name="flipped", bufs=1))
        stack.enter_context(tc.manual_schedule())

        def tile_rows(tensor, t):
            return tensor.rearrange("b (k t) c -> t (b k) c", t=TOKEN_TILES)[t]

        identity = keep.tile([P, P], F32)
        make_identity(nc, identity[:])
        nullary = keep.tile([P, CH], BF16)
        nc.vector.memset(nullary[:].bitcast(I32), 0)
        table_loaded = keep.tile([P, 1], F32)
        nc.scalar.activation(out=table_loaded[:], in_=nullary[:, 0:1], func=ACT.Sigmoid)
        ones = keep.tile([P, P], BF16)
        nc.gpsimd.memset(ones[:], 1.0)
        bias_row = keep.tile([P, OUT], BF16)
        nc.gpsimd.memset(bias_row[:].bitcast(I32), 0)
        bias_rows = keep.tile([P, P], F32)
        nc.gpsimd.memset(bias_rows[:], 0.0)
        without_flat = keep.tile([P, TILE_OBJECTS * (P + 1)], F32)
        without = without_flat[:, 0 : TILE_OBJECTS * P].rearrange("p (s k) -> p s k", k=P)
        nc.vector.tensor_copy(out=without, in_=identity[:].unsqueeze(1).to_broadcast([P, TILE_OBJECTS, P]))
        nc.vector.memset(diagonal(without_flat, P, 1), 0.0)
        w_scales = keep.tile([P, GROUPS, OUT], U8, align_bytes=64)
        nc.vector.memset(w_scales[:].rearrange("p g n -> p (g n)").bitcast(I32), 0)

        relations = [keep.tile([P, OBJECTS, CH], BF16, name="relations_%d" % t) for t in range(TOKEN_TILES)]

        def load_relations(t, first, count):
            rows = tile_rows(x2.rearrange("b i j c -> b i (j c)"), t)
            nc.sync.dma_start(
                out=relations[t][:, first : first + count, :].rearrange("p j c -> p (j c)"),
                in_=rows[:, first * CH : (first + count) * CH],
            )

        head = [keep.tile([P, 2, CH], BF16, name="head_%d" % k) for k in range(CHUNK)]

        def load_head(c, is_far):
            rows = x2.rearrange("b (k t) (j f) c -> t f (b k) j c", t=TOKEN_TILES, f=2)[0, is_far]
            nc.sync.dma_start(out=head[2 * c + is_far][:], in_=rows[:, 2 * c : 2 * c + 2, :])

        w_words = [keep.tile([P, GROUPS, 2 * N_TILE], U8, name="w_words_%d" % n, align_bytes=64) for n in range(N_TILES)]

        def load_weights(n):
            cols = slice(2 * n * N_TILE, 2 * (n + 1) * N_TILE)
            nc.sync.dma_start(
                out=w_words[n][:].bitcast(I32), in_=W1_words[:, :, cols].rearrange("g p n -> p g n").bitcast(I32)
            )

        for c in range(2):
            load_head(c, 1)
            load_head(c, 0)
        nc.sync.dma_start(out=bias_row[0:1, :], in_=b1.unsqueeze(0))
        for c in range(2, CHUNKS):
            load_relations(0, c * CHUNK, CHUNK)
        bias_short = keep.tile([OUT // P, P], BF16)
        nc.sync.dma_start(out=bias_short[:], in_=b1.rearrange("(m k) -> m k", k=P))
        nc.sync.dma_start(out=nullary[0:SCENES, :], in_=x0)
        unary = keep.tile([P, TOKEN_TILES, CH], BF16)
        for t in range(TOKEN_TILES):
            nc.sync.dma_start(out=unary[:, t, :], in_=tile_rows(x1, t))
        for r in range(4):
            nc.sync.dma_start(
                out=w_scales[r:P:32, :, :].bitcast(I32),
                in_=W1_scales[:, r:16:4, :].rearrange("g q n -> q g n").bitcast(I32),
            )
        load_weights(0)
        for c in range(CHUNKS):
            load_relations(1, c * CHUNK, CHUNK)
        for n in range(1, N_TILES):
            load_weights(n)

        def turn(src, bank_part, selector):
            for u in range(WORD_HALVES):
                nc.tensor.transpose(bank_part[:, u, :], src.bitcast(F32)[:, u : CH // 2 : WORD_HALVES], selector)

        def turn_two(two, selectors, dst):
            bank = banks.tile([P, BANK_ROWS, WORD_HALVES, P], F32, tag="bank")
            for s in range(BANK_ROWS):
                turn(two[s], bank[:, s, :, :], selectors[s])
            nc.scalar.copy(
                out=dst.bitcast(F32).rearrange("p s (k u) -> p s k u", u=WORD_HALVES),
                in_=bank[:].rearrange("p s u k -> p s k u"),
            )

        near_flat = [
            keep.tile([P, TILE_OBJECTS * (CH + PACK)], BF16, name="near_%d" % t) for t in range(TOKEN_TILES)
        ]
        far_turned = keep.tile([P, TOKEN_TILES, len(KINDS), CH], BF16)

        def near(t, first, count):
            return near_flat[t][:, first * CH : (first + count) * CH].rearrange("p (s k) -> p s k", k=CH)

        def far(t, first, count):
            if t == 0 and first < CHUNK:
                return head[first + 1][:]
            j = 2 * first + 1 - t
            return relations[t][:, j : j + 2 * count - 1 : 2, :]

        def turn_near(t, c):
            s = c * BANK_ROWS
            turn_two(
                [head[s][:, k, :] if t == 0 and c < 2 else relations[t][:, 2 * (s + k) + t, :] for k in range(BANK_ROWS)],
                [without[:, s + k, :] for k in range(BANK_ROWS)],
                near(t, s, BANK_ROWS),
            )

        def turn_far(t, reduced):
            turn_two([reduced[k] for k in KINDS], [identity[:]] * BANK_ROWS, far_turned[:, t, :, :])

        f1 = keep.tile([P, SLOTS, CH], BF16, align_bytes=64)
        f1_words = keep.tile([P, SLOTS, P], U32, align_bytes=64)
        f1_scales = keep.tile([P, SLOTS, P], U8, align_bytes=64)

        def turn_inputs():
            scene_words = banks.tile([P, WORD_HALVES, P], F32, tag="bank")
            turn(nullary[:], scene_words, identity[:])
            nc.scalar.copy(
                out=f1[:, f1_slot(0, 0), :].bitcast(F32).rearrange(
                    "p (b i u) -> p b i u", i=TILE_OBJECTS, u=WORD_HALVES
                ),
                in_=scene_words[:, :, 0:SCENES]
                .rearrange("p u b -> p b u")
                .unsqueeze(2)
                .to_broadcast([P, SCENES, TILE_OBJECTS, WORD_HALVES]),
            )
            first = f1_slot(1, 0)
            turn_two(
                [unary[:, t, :] for t in range(TOKEN_TILES)],
                [identity[:]] * BANK_ROWS,
                f1[:, first : first + TOKEN_TILES, :],
            )

        bias_columns = keep.tile([P, OUT // P], F32)

        def turn_bias():
            nc.scalar.copy(out=bias_rows[0 : OUT // P, :], in_=bias_short[:])
            bias_words = banks.tile([P, P], F32, tag="bank")
            nc.tensor.transpose(bias_words[:], bias_rows[:], identity[:])
            nc.scalar.copy(out=bias_columns[:], in_=bias_words[:, 0 : OUT // P])

        bias = keep.tile([P, OUT], BF16)

        def spread_bias(n):
            cols = slice(n * N_TILE, (n + 1) * N_TILE)
            bank = sums_0.tile([P, N_TILE], F32, tag="bank")
            nc.tensor.matmul(bank[:], lhsT=ones[:], rhs=bias_row[:, cols], start=True, stop=True)
            nc.scalar.copy(out=bias[:, cols], in_=bank[:])

        def quantise(first, count):
            slots = slice(first, first + count)
            nc.vector.quantize_mx(
                out=f1_words[:, slots, :].rearrange("p q m -> p (q m)").bitcast(FP8X4),
                scales=f1_scales[:, slots, :].rearrange("p q m -> p (q m)"),
                in_=f1[:, slots, :].rearrange("p q k -> p (q k)"),
            )

        def best_of(kind, dst, a, b):
            nc.vector.tensor_tensor(out=dst, in0=a, in1=b, op=OPS[kind])

        def refill(t, first, count):
            nc.gpsimd.memset(diagonal(near_flat[t], CH, PACK)[:, first : first + count, :, :], 1.0)

        def scratch(t, label, rows):
            return [keep.tile([P, rows, CH], BF16, name="%s_%d_%d" % (label, t, k)) for k in KINDS]

        sums = {}

        def one_pass(t, g, n):
            if g == 0:
                pool = sums_0 if t == 0 else sums_1 if n < EARLY else banks
                bank = pool.tile([P, N_TILE], F32, tag="bank")
                sums[(t, n)] = bank
            slot = f1_slot(g, t)
            nc.tensor.matmul_mx(
                out=sums[(t, n)][:],
                lhsT=f1_words[:, slot, :].bitcast(FP8X4),
                lhsT_scale=f1_scales[:, slot, :],
                rhs=w_words[n][:, g, :].bitcast(FP4X4),
                rhs_scale=w_scales[:, g, n * N_TILE : (n + 1) * N_TILE],
                start=(g == 0),
                stop=(g == GROUPS - 1),
            )

        def flipped_passes(n):
            bank = flipped.tile([P, N_TILE // P, P], F32, tag="bank")
            for m in range(N_TILE // P):
                first = n * N_TILE + m * P
                for g in range(GROUPS):
                    slot = f1_slot(g, 0)
                    nc.tensor.matmul_mx(
                        out=bank[:, m, :],
                        lhsT=w_words[n][:, g, 2 * m * P : 2 * (m + 1) * P].bitcast(FP4X4),
                        lhsT_scale=w_scales[:, g, first : first + P],
                        rhs=f1_words[:, slot, :].bitcast(FP8X4),
                        rhs_scale=f1_scales[:, slot, :],
                        start=(g == 0),
                        stop=(g == GROUPS - 1),
                    )
            sums[(0, n)] = bank

        activated = {}

        def flipped_sigmoids(n):
            result = keep.tile([P, N_TILE // P, P], F32, name="activated_%d" % n)
            for m in range(N_TILE // P):
                column = n * (N_TILE // P) + m
                nc.scalar.activation(
                    out=result[:, m, :],
                    in_=sums[(0, n)][:, m, :],
                    func=ACT.Sigmoid,
                    bias=bias_columns[:, column : column + 1],
                )
            activated[n] = result

        def flip_back(n):
            bank = flipped.tile([P, N_TILE // P, P], F32, tag="bank")
            for m in range(N_TILE // P):
                nc.tensor.transpose(bank[:, m, :], activated[n][:, m, :], identity[:])
            result = keep.tile([P, N_TILE], F32, name="result_0_%d" % n)
            nc.scalar.copy(out=result[:], in_=bank[:].rearrange("p m k -> p (m k)"))
            cols = slice(n * N_TILE, (n + 1) * N_TILE)
            nc.sync.dma_start(out=tile_rows(out, 0)[:, cols], in_=result[:])

        def finish(t, n, parts=1):
            width = N_TILE // parts
            result = keep.tile([P, N_TILE], F32, name="result_%d_%d" % (t, n))
            for first in range(0, N_TILE, width):
                part = result[:, first : first + width]
                cols = slice(n * N_TILE + first, n * N_TILE + first + width)
                nc.vector.tensor_tensor(
                    out=part, in0=sums[(t, n)][:, first : first + width], in1=bias[:, cols], op=ALU.add
                )
                nc.scalar.activation(out=part, in_=part, func=ACT.Sigmoid)
                nc.sync.dma_start(out=tile_rows(out, t)[:, cols], in_=part)


        def fold(k, dst, src):
            half = src.shape[1] // 2
            best_of(k, dst, src[:, 0:half, :], src[:, half : 2 * half, :])

        def whole(t, k, near_best, far_best_turned):
            best_of(k, f1[:, f1_slot(2 + k, t), :], near_best[k][:, 0, :], far_best_turned)

        far_pairs = scratch(0, "far_pairs", CHUNKS)
        near_pairs = scratch(0, "near_pairs", CHUNKS)
        far_fours = scratch(0, "far_fours", 2)
        near_fours = scratch(0, "near_fours", 2)
        far_best = scratch(0, "far_best", 1)
        near_best = scratch(0, "near_best", 1)

        def far_pair(c):
            for k in KINDS:
                fold(k, far_pairs[k][:, c : c + 1, :], far(0, 2 * c, 2))

        def near_pair(k, c, count=1):
            fold(k, near_pairs[k][:, c : c + count, :], near(0, 2 * c, 2 * count))
            if k == MAX:
                refill(0, 2 * c, 2 * count)

        def far_four(h):
            for k in KINDS:
                fold(k, far_fours[k][:, h : h + 1, :], far_pairs[k][:, 2 * h : 2 * h + 2, :])

        for c in range(CHUNKS):
            turn_near(0, c)
        turn_inputs()
        far_pair(0)
        far_pair(1)
        far_four(0)
        near_pair(MAX, 0)
        far_pair(2)
        near_pair(MAX, 1)
        near_pair(MIN, 0)
        far_pair(3)
        near_pair(MIN, 1)
        far_four(1)
        near_pair(MAX, 2, 2)
        for k in KINDS:
            fold(k, far_best[k][:], far_fours[k][:])
        quantise(f1_slot(0, 0), 1)
        near_pair(MIN, 2, 2)
        quantise(f1_slot(1, 0), TOKEN_TILES)

        def early_passes(t, n):
            for g in range(2):
                one_pass(t, g, n)

        def late_passes(t, n):
            for g in range(2, GROUPS):
                one_pass(t, g, n)

        turn_far(0, [far_best[k][:, 0, :] for k in KINDS])
        early_passes(1, 0)
        turn_bias()
        for c in range(2):
            turn_near(1, c)
            spread_bias(c)
        for k in KINDS:
            fold(k, near_fours[k][:], near_pairs[k][:])
        for k in KINDS:
            fold(k, near_best[k][:], near_fours[k][:])
        for k in KINDS:
            whole(0, k, near_best, far_turned[:, 0, k, :])

        far_fours = scratch(1, "far_fours", 4)
        near_fours = scratch(1, "near_fours", 4)
        far_pairs = scratch(1, "far_pairs", 2)
        near_pairs = scratch(1, "near_pairs", 2)
        far_best = scratch(1, "far_best", 1)
        near_best = scratch(1, "near_best", 1)

        def far_half(k, h):
            fold(k, far_fours[k][:, 2 * h : 2 * h + 2, :], far(1, 4 * h, 4))

        def near_half(k, h):
            fold(k, near_fours[k][:, 2 * h : 2 * h + 2, :], near(1, 4 * h, 4))
            if k == MAX:
                refill(1, 4 * h, 4)

        far_half(MAX, 0)
        quantise(f1_slot(2, 0), len(KINDS))
        far_half(MIN, 0)
        spread_bias(2)
        flipped_passes(0)
        spread_bias(3)
        turn_near(1, 2)
        flipped_sigmoids(0)
        turn_near(1, 3)
        near_half(MAX, 0)
        early_passes(1, 1)
        early_passes(0, 1)
        late_passes(0, 1)
        flip_back(0)
        for k in KINDS:
            far_half(k, 1)
        near_half(MIN, 0)
        for k in KINDS:
            fold(k, far_pairs[k][:], far_fours[k][:])
        near_half(MAX, 1)
        for k in KINDS:
            fold(k, far_best[k][:], far_pairs[k][:])
        early_passes(0, 2)
        turn_far(1, [far_best[k][:, 0, :] for k in KINDS])
        late_passes(0, 2)
        early_passes(0, 3)
        late_passes(0, 3)
        for n in range(2, N_TILES):
            early_passes(1, n)
        fold(MAX, near_pairs[MAX][:], near_fours[MAX][:])
        near_half(MIN, 1)
        finish(0, 1)
        fold(MAX, near_best[MAX][:], near_pairs[MAX][:])
        fold(MIN, near_pairs[MIN][:], near_fours[MIN][:])
        whole(1, MAX, near_best, far_turned[:, 1, MAX, :])
        fold(MIN, near_best[MIN][:], near_pairs[MIN][:])
        quantise(f1_slot(2, 1), 1)
        whole(1, MIN, near_best, far_turned[:, 1, MIN, :])
        finish(0, 2)
        quantise(f1_slot(3, 1), 1)
        for g in range(2, GROUPS):
            for n in range(N_TILES):
                one_pass(1, g, n)
        finish(0, 3)
        for n in range(N_TILES):
            finish(1, n, 2 if n == N_TILES - 1 else 1)
